import numpy as np
import ml_dtypes


def mxq(x, axis, fmt="e4m3"):
    dtype, down = {"e4m3": (ml_dtypes.float8_e4m3fn, 7), "e5m2": (ml_dtypes.float8_e5m2, 14)}[fmt]
    v = np.moveaxis(np.asarray(x, np.float32).astype(ml_dtypes.bfloat16).astype(np.float64), axis, -1)
    blocks = v.reshape(v.shape[:-1] + (-1, 32))
    amax = np.abs(blocks).max(-1, keepdims=True)
    byte = np.maximum(np.where(amax > 0, np.frexp(amax)[1] - 1 + 127, 0) - down, 1)
    scale = np.exp2(byte - 127.0)
    codes = (blocks / scale).astype(np.float32).astype(dtype).astype(np.float64)
    return np.moveaxis((codes * scale).reshape(v.shape), -1, axis)


WIDE = False


def mx_kscale(k):
    if not WIDE:
        return np.ones(k)
    levels = np.array([10, -10, 5, -5, 0])
    a = np.random.permutation(np.resize(levels, k // 512 * 4)).reshape(k // 512, 4)
    idx = np.arange(k)
    return np.exp2(a[idx // 512, idx % 128 // 32])


BF16 = ml_dtypes.bfloat16


def bf(x):
    return np.asarray(x, np.float32).astype(BF16)


def f64(x):
    return np.asarray(x).astype(np.float64)


B, N1, N2, D, H, DH = 4, 512, 512, 256, 2, 256
HD = H * DH
N = N1 + N2


def setup_inputs():
    t = mx_kscale(HD)
    tv = t.reshape(H, 1, DH)
    sgn = np.where(np.random.standard_normal((H, 1, DH)) < 0.0, -1.0, 1.0)
    return {"q_rot": bf(np.random.standard_normal((B, H, N, DH)) * 1.2),
            "k_rot": bf(np.random.standard_normal((B, H, N, DH)) * 1.2),
            "v": bf(np.abs(np.random.standard_normal((B, H, N, DH))) * sgn * tv),
            "w_out1": bf(np.random.standard_normal((HD, D)) * 1.5 / np.sqrt(HD) / t[:, None]),
            "b_out1": bf(np.random.standard_normal(D) * 0.1),
            "w_out2": bf(np.random.standard_normal((HD, D)) * 1.5 / np.sqrt(HD) / t[:, None]),
            "b_out2": bf(np.random.standard_normal(D) * 0.1)}


def reference(q_rot, k_rot, v, w_out1, b_out1, w_out2, b_out2):
    s = f64(q_rot) @ f64(k_rot).transpose(0, 1, 3, 2) * (1.0 / np.sqrt(DH))
    e = np.exp(s - s.max(-1, keepdims=True))
    attn = (mxq(e, 3, "e4m3") @ mxq(f64(v), 2, "e4m3")) / e.sum(-1, keepdims=True)
    attn = attn.transpose(0, 2, 1, 3).reshape(B, N, HD)
    out1 = (mxq(attn[:, :N1], 2, "e4m3") @ mxq(f64(w_out1), 0, "e4m3")) + f64(b_out1)
    out2 = (mxq(attn[:, N1:], 2, "e4m3") @ mxq(f64(w_out2), 0, "e4m3")) + f64(b_out2)
    return out1, out2

@@ -1,0 +1,446 @@
+from contextlib import ExitStack
+
+import concourse.mybir as mybir
+from concourse.masks import make_identity
+
+F32 = mybir.dt.float32
+BF16 = mybir.dt.bfloat16
+U32 = mybir.dt.uint32
+U8 = mybir.dt.uint8
+FP8X4 = mybir.dt.float8_e4m3fn_x4
+ACT = mybir.ActivationFunctionType
+ALU = mybir.AluOpType
+AX = mybir.AxisListType
+
+B, H, N, DH, D = 4, 2, 1024, 256, 256
+P = 128
+SCALE = 1.0 / 16.0
+FLOPS = 2 * B * H * N * N * DH * 2 + 2 * B * N * H * DH * D
+
+UNITS = B * 8 * H
+PAIRS = UNITS // 2
+MANUAL = True
+G_E = False
+G_K = False
+OFF_G, OFF_H, OFF_J, OFF_L, OFF_M = 4, 7, 10, 11, 13
+QK_V = 2
+I_S_EVERY = 4
+TAIL_S = True
+
+
+def tile_mmattn_pb_t_kernel(tc, q_rot, k_rot, v, w_out1, b_out1, w_out2, b_out2, out_0, out_1):
+    nc = tc.nc
+    outs = [out_0, out_1]
+    srcs = {"q": q_rot, "k": k_rot, "v": v}
+    with ExitStack() as ctx:
+        consts = ctx.enter_context(tc.tile_pool(name="consts", bufs=1))
+        raw = ctx.enter_context(tc.tile_pool(name="raw", bufs=2))
+        xt = ctx.enter_context(tc.tile_pool(name="xt", bufs=2))
+        vq = ctx.enter_context(tc.tile_pool(name="vq", bufs=2))
+        ep = ctx.enter_context(tc.tile_pool(name="ep", bufs=4))
+        gp = ctx.enter_context(tc.tile_pool(name="gp", bufs=3))
+        g1 = ctx.enter_context(tc.tile_pool(name="g1", bufs=1))
+        st4 = ctx.enter_context(tc.tile_pool(name="st4", bufs=6))
+        ap3 = ctx.enter_context(tc.tile_pool(name="ap3", bufs=3))
+        ps_s = ctx.enter_context(tc.psum_pool(name="ps_s", bufs=4))
+        ps_t = ctx.enter_context(tc.psum_pool(name="ps_t", bufs=2))
+        ps_m = ctx.enter_context(tc.psum_pool(name="ps_m", bufs=2))
+        if MANUAL:
+            ctx.enter_context(tc.manual_schedule())
+
+        ident_f = consts.tile([P, P], F32)
+        make_identity(nc, ident_f[:])
+        ident_b = consts.tile([P, P], BF16)
+        make_identity(nc, ident_b[:])
+
+        raws = {}
+
+        def load(x, b, h, halves):
+            if (x, b, h) not in raws:
+                t = raw.tile([P, 2, 4, DH], BF16, name="raw_%s%d" % (x, h))
+                raws[(x, b, h)] = t
+            t = raws[(x, b, h)]
+            if x == "q":
+                view = srcs[x][b, h].rearrange("(a c p) d -> p a c d", a=2, c=4)
+            else:
+                view = srcs[x][b, h].rearrange("(a p c) d -> p a c d", a=2, c=4)
+            if len(halves) == 2:
+                nc.sync.dma_start(out=t[:], in_=view)
+            else:
+                a = halves[0]
+                nc.sync.dma_start(out=t[:, a], in_=view[:, a])
+
+        def load_batch(b):
+            for h in range(H):
+                load("k", b, h, (0, 1))
+                load("q", b, h, (0, 1))
+            for h in range(H):
+                load("v", b, h, (0, 1))
+
+        for h in range(H):
+            load("k", 0, h, (0,))
+            load("k", 0, h, (1,))
+            load("q", 0, h, (0,))
+        for h in range(H):
+            load("v", 0, h, (0, 1))
+        load("k", 1, 0, (0, 1))
+        for h in range(H):
+            load("q", 0, h, (1,))
+        load("q", 1, 0, (0, 1))
+        w_raw = consts.tile([P, 2, 4, D], BF16)
+        bias_bf = consts.tile([P, 2, D], BF16)
+        for s, (w, bb) in enumerate(((w_out1, b_out1), (w_out2, b_out2))):
+            nc.sync.dma_start(out=w_raw[:, s], in_=w.rearrange("(j p) o -> p j o", p=P))
+            nc.sync.dma_start(out=bias_bf[:, s, :], in_=bb.partition_broadcast(P))
+        load("k", 1, 1, (0, 1))
+        load("q", 1, 1, (0, 1))
+        for h in range(H):
+            load("v", 1, h, (0, 1))
+
+        w_grp = consts.tile([P, 2, D, 4], BF16, align_bytes=64)
+        w_codes = consts.tile([P, 2, D], U32, align_bytes=64)
+        w_scales = consts.tile([P, 2, D], U8, align_bytes=64)
+        bias_f = consts.tile([P, 2, D], F32)
+
+        def prep_w():
+            for s in range(2):
+                nc.vector.tensor_copy(out=w_grp[:, s], in_=w_raw[:, s].rearrange("p j o -> p o j"))
+            nc.vector.tensor_copy(out=bias_f[:], in_=bias_bf[:])
+            nc.vector.quantize_mx(
+                out=w_codes[:].rearrange("p s o -> p (s o)").bitcast(FP8X4),
+                scales=w_scales[:].rearrange("p s o -> p (s o)"),
+                in_=w_grp[:].rearrange("p s o j -> p (s o j)"),
+            )
+
+        def copy_on(eng, out, in_):
+            if eng == "v":
+                nc.vector.tensor_copy(out=out, in_=in_)
+            else:
+                nc.scalar.copy(out=out, in_=in_)
+
+        def misc_bank(st, shape, dtype, name):
+            if st >= UNITS + 2:
+                return ps_s.tile(shape, dtype, name=name, tag="s_ps")
+            return ps_m.tile(shape, dtype, name=name, tag="m")
+
+        xts = {}
+
+        def qk_group(st, x, b, h, a):
+            src = raws[(x, b, h)]
+            if (x, b, h) not in xts:
+                t = xt.tile([P, 8 * P], F32, name="xt_%s%d" % (x, h))
+                xts[(x, b, h)] = t
+            dst = xts[(x, b, h)]
+            bank = misc_bank(st, [P, 4, P], F32, "bank_x")
+            trs = [
+                (lambda c=c: nc.tensor.transpose(bank[:, c, :], src[:, a, c, :].bitcast(F32), ident_f[:]))
+                for c in range(4)
+            ]
+            return trs, lambda eng: copy_on(eng, dst[:, a * 512:(a + 1) * 512], bank[:].rearrange("p c t -> p (c t)"))
+
+        GROUPS = [("k", 0, 0), ("k", 0, 1), ("q", 0, 0), ("k", 1, 0), ("k", 1, 1), ("q", 1, 0), ("q", 0, 1), ("q", 1, 1)]
+        qk_plan = {0: [(0, 3), (0, 4), (0, 5)], 4: [(0, 6)], 6: [(0, 7)]}
+        for b in range(1, B):
+            for n in range(8):
+                step = 16 * (b - 1) + 2 * n + 2
+                qk_plan[step] = qk_plan.get(step, []) + [(b, n)]
+
+        def half(view, e):
+            return view.bitcast(BF16).rearrange("p (x e) -> p x e", e=2)[:, :, e]
+
+        vcs = {}
+
+        def v_regroup(b, h, g):
+            if g == 0:
+                v_grp = vq.tile([P, 2, DH, 4], BF16, name="v_grp%d" % h, align_bytes=64)
+                vcs[("g", b, h)] = v_grp
+            v_grp = vcs[("g", b, h)]
+            nc.gpsimd.tensor_scalar(
+                out=v_grp[:, g], in0=raws[("v", b, h)][:, g].rearrange("p j d -> p d j"),
+                scalar1=1.0, scalar2=0.0, op0=ALU.mult, op1=ALU.add,
+            )
+
+        def v_quant(b, h):
+            v_codes = vq.tile([P, 2 * DH], U32, name="v_codes%d" % h, align_bytes=64)
+            v_scales = vq.tile([P, 2 * DH], U8, name="v_scales%d" % h, align_bytes=64)
+            nc.vector.quantize_mx(
+                out=v_codes[:].bitcast(FP8X4), scales=v_scales[:],
+                in_=vcs[("g", b, h)][:].rearrange("p g d j -> p (g d j)"),
+            )
+            vcs[("c", b, h)] = (v_codes, v_scales)
+
+        live = {}
+
+        def stage_a(i):
+            b, r = divmod(i, 16)
+            t, h = divmod(r, 2)
+            qt = xts[("q", b, h)]
+            kt = xts[("k", b, h)]
+            banks = []
+            mms = []
+            for g in range(2):
+                s_ps = ps_s.tile([P, 512], F32, name="s_ps")
+                banks.append(s_ps)
+                for e in range(2):
+                    mms.append(
+                        lambda s_ps=s_ps, g=g, e=e: nc.tensor.matmul(
+                            out=s_ps[:],
+                            lhsT=half(qt[:, t * P:(t + 1) * P], e),
+                            rhs=half(kt[:, g * 512:(g + 1) * 512], e),
+                            start=(e == 0), stop=(e == 1),
+                        )
+                    )
+            live[("s", i)] = banks
+            return mms
+
+        def stage_b(i):
+            banks = live[("s", i)]
+            m2 = st4.tile([P, 2], F32, name="m2")
+            for g in range(2):
+                nc.vector.reduce_max(out=m2[:, g:g + 1], in_=banks[g][:], axis=AX.X)
+            negmax = st4.tile([P, 1], F32, name="negmax")
+            nc.vector.tensor_scalar(
+                out=negmax[:], in0=m2[:, 0:1], scalar1=m2[:, 1:2], scalar2=-SCALE, op0=ALU.max, op1=ALU.mult
+            )
+            live[("negmax", i)] = negmax
+
+        def stage_c(i):
+            banks = live[("s", i)]
+            negmax = live[("negmax", i)]
+            if i % 2 == 0:
+                rs = st4.tile([P, 4], F32, name="rs")
+                live[("rs", i // 2)] = rs
+            rs = live[("rs", i // 2)]
+            e_sb = ep.tile([P, 8, P], BF16, name="e_sb")
+            for g in range(2):
+                col = (i % 2) * 2 + g
+                nc.scalar.activation(
+                    out=e_sb[:, 4 * g:4 * g + 4, :].rearrange("p j m -> p (j m)"), in_=banks[g][:], func=ACT.Exp,
+                    bias=negmax[:, 0:1], scale=SCALE, accum_out=rs[:, col:col + 1],
+                )
+            live[("e", i)] = e_sb
+
+        def stage_d(i):
+            e_sb = live[("e", i)]
+            et_ps = ps_t.tile([P, 8, P], BF16, name="et_ps")
+            live[("et", i)] = et_ps
+            return [
+                (lambda x=x: nc.tensor.transpose(et_ps[:, x, :], e_sb[:, x, :], ident_b[:])) for x in range(8)
+            ]
+
+        def stage_e(i, eng):
+            et_ps = live[("et", i)]
+            if G_E and i % 2 == 1:
+                et_raw = gp.tile([P, 8, P], BF16, name="et_raw")
+                copy_on(eng, et_raw[:], et_ps[:])
+                live[("etr", i)] = et_raw
+            else:
+                eg = gp.tile([P, 2, P, 4], BF16, name="eg%d" % (i % 2), align_bytes=64)
+                copy_on(eng, eg[:], et_ps[:].rearrange("p (g j) q -> p g q j", j=4))
+                live[("eg", i)] = eg
+
+        def stage_f(i):
+            et_raw = live[("etr", i)]
+            eg = g1.tile([P, 2, P, 4], BF16, name="eg_g", align_bytes=64)
+            nc.gpsimd.tensor_scalar(
+                out=eg[:], in0=et_raw[:].rearrange("p (g j) q -> p g q j", j=4),
+                scalar1=1.0, scalar2=0.0, op0=ALU.mult, op1=ALU.add,
+            )
+            live[("eg", i)] = eg
+
+        def stage_gq(u):
+            rs = live[("rs", u)]
+            e_codes = gp.tile([P, 4 * P], U32, name="e_codes", align_bytes=64)
+            e_scales = gp.tile([P, 4 * P], U8, name="e_scales", align_bytes=64)
+            for h in range(H):
+                nc.vector.quantize_mx(
+                    out=e_codes[:, h * 256:(h + 1) * 256].bitcast(FP8X4), scales=e_scales[:, h * 256:(h + 1) * 256],
+                    in_=live[("eg", 2 * u + h)][:].rearrange("p g q j -> p (g q j)"),
+                )
+            rsum = st4.tile([P, 2], F32, name="rsum")
+            nc.vector.tensor_reduce(out=rsum[:], in_=rs[:].rearrange("p (h g) -> p h g", g=2), axis=AX.X, op=ALU.add)
+            rinv = st4.tile([P, 2], F32, name="rinv")
+            nc.vector.reciprocal(out=rinv[:], in_=rsum[:])
+            live[("ec", u)] = (e_codes, e_scales, rinv)
+
+        def stage_h(st, u):
+            b = u // 8
+            e_codes, e_scales, rinv = live[("ec", u)]
+            pv = misc_bank(st, [P, 2, DH], F32, "pv")
+            live[("pv", u)] = pv
+            mx = []
+            for h in range(H):
+                v_codes, v_scales = vcs[("c", b, h)]
+                for g in range(2):
+                    c0 = (h * 2 + g) * P
+                    mx.append(
+                        lambda h=h, g=g, c0=c0, v_codes=v_codes, v_scales=v_scales: nc.tensor.matmul_mx(
+                            out=pv[:, h, :],
+                            lhsT=e_codes[:, c0:c0 + P].bitcast(FP8X4), lhsT_scale=e_scales[:, c0:c0 + P],
+                            rhs=v_codes[:, g * DH:(g + 1) * DH].bitcast(FP8X4),
+                            rhs_scale=v_scales[:, g * DH:(g + 1) * DH],
+                            start=(g == 0), stop=(g == 1),
+                        )
+                    )
+            return mx
+
+        def stage_i(u, eng):
+            pv = live[("pv", u)]
+            rinv = live[("ec", u)][2]
+            attn = ap3.tile([P, H * DH], BF16, name="attn")
+            live[("attn", u)] = attn
+            for h in range(H):
+                if eng == "v":
+                    nc.vector.tensor_scalar(
+                        out=attn[:, h * DH:(h + 1) * DH], in0=pv[:, h, :], scalar1=rinv[:, h:h + 1], scalar2=None,
+                        op0=ALU.mult,
+                    )
+                else:
+                    nc.scalar.activation(
+                        out=attn[:, h * DH:(h + 1) * DH], in_=pv[:, h, :], func=ACT.Copy, scale=rinv[:, h:h + 1]
+                    )
+
+        def stage_j(st, u):
+            attn = live[("attn", u)]
+            at_ps = misc_bank(st, [P, 4, P], BF16, "at_ps")
+            live[("at", u)] = at_ps
+            return [
+                (lambda j=j: nc.tensor.transpose(at_ps[:, j, :], attn[:, j * P:(j + 1) * P], ident_b[:]))
+                for j in range(4)
+            ]
+
+        def stage_k(u, eng):
+            at_ps = live[("at", u)]
+            if G_K:
+                at_raw = ap3.tile([P, 4, P], BF16, name="at_raw")
+                copy_on(eng, at_raw[:], at_ps[:])
+                live[("atr", u)] = at_raw
+            else:
+                ag = ap3.tile([P, P, 4], BF16, name="ag", align_bytes=64)
+                copy_on(eng, ag[:], at_ps[:].rearrange("p j q -> p q j"))
+                live[("ag", u)] = ag
+
+        def stage_k2(u):
+            at_raw = live[("atr", u)]
+            ag = g1.tile([P, P, 4], BF16, name="ag_g", align_bytes=64)
+            nc.gpsimd.tensor_scalar(
+                out=ag[:], in0=at_raw[:].rearrange("p j q -> p q j"), scalar1=1.0, scalar2=0.0, op0=ALU.mult, op1=ALU.add
+            )
+            live[("ag", u)] = ag
+
+        def stage_l(u):
+            ag = live[("ag", u)]
+            a_codes = ap3.tile([P, P], U32, name="a_codes", align_bytes=64)
+            a_scales = ap3.tile([P, P], U8, name="a_scales", align_bytes=64)
+            nc.vector.quantize_mx(
+                out=a_codes[:].bitcast(FP8X4), scales=a_scales[:], in_=ag[:].rearrange("p q j -> p (q j)")
+            )
+            live[("ac", u)] = (a_codes, a_scales)
+
+        def stage_m(st, u):
+            s = (u % 8) // 4
+            a_codes, a_scales = live[("ac", u)]
+            o_ps = misc_bank(st, [P, D], F32, "o_ps")
+            live[("o", u)] = o_ps
+            return [
+                lambda: nc.tensor.matmul_mx(
+                    out=o_ps[:],
+                    lhsT=a_codes[:].bitcast(FP8X4), lhsT_scale=a_scales[:],
+                    rhs=w_codes[:, s, :].bitcast(FP8X4), rhs_scale=w_scales[:, s, :],
+                    start=True, stop=True,
+                )
+            ]
+
+        def stage_n(u):
+            b = u // 8
+            s = (u % 8) // 4
+            o_ps = live[("o", u)]
+            o_sb = ap3.tile([P, D], F32, name="o_sb", bufs=8)
+            nc.vector.tensor_tensor(out=o_sb[:], in0=o_ps[:], in1=bias_f[:, s, :], op=ALU.add)
+            nc.sync.dma_start(out=outs[s][b, (u % 4) * P:(u % 4 + 1) * P, :], in_=o_sb[:])
+
+        def weave(mms, ds, mxs, ts):
+            per = 3
+            pos = 0
+            for mm in mms:
+                mm()
+                for f in ds[pos:pos + per]:
+                    f()
+                pos += per
+            for f in ds[pos:] + mxs + ts:
+                f()
+
+        def due(st, off):
+            if st >= off and (st - off) % 2 == 0 and (st - off) // 2 < PAIRS:
+                return (st - off) // 2
+            return None
+
+        for n in range(3):
+            x, h, a = GROUPS[n]
+            trs, evac = qk_group(0, x, 0, h, a)
+            for f in trs:
+                f()
+            evac("v" if n % 2 == 0 else "s")
+
+        for st in range(UNITS + OFF_M - 1):
+            b16, r16 = divmod(st, 16)
+            tail = TAIL_S and st >= UNITS
+            mms, ds, mxs, ts = [], [], [], []
+            post_s, post_v = [], []
+            if st < UNITS:
+                mms = stage_a(st)
+            if r16 == 4 and b16 + 2 < B:
+                load_batch(b16 + 2)
+            if st == 6:
+                post_v.append(prep_w)
+            if 0 <= st - 2 < UNITS:
+                ds += stage_d(st - 2)
+                if tail and st % 2 == 1:
+                    post_v.append(lambda: stage_e(st - 2, "v"))
+                else:
+                    post_s.append(lambda: stage_e(st - 2, "s"))
+            if st < UNITS and r16 < 4:
+                v_regroup(b16, r16 // 2, r16 % 2)
+            if st < UNITS and r16 in (2, 4):
+                post_v.append(lambda: v_quant(b16, r16 // 2 - 1))
+            for n, (b, gi) in enumerate(qk_plan.get(st, [])):
+                x, h, a = GROUPS[gi]
+                trs, evac = qk_group(st, x, b, h, a)
+                ts += trs
+                if (st % 4 == QK_V) == (n % 2 == 0):
+                    post_v.append(lambda evac=evac: evac("v"))
+                else:
+                    post_s.append(lambda evac=evac: evac("s"))
+            ug, uh, uj, ul, um = due(st, OFF_G), due(st, OFF_H), due(st, OFF_J), due(st, OFF_L), due(st, OFF_M)
+            if ug is not None:
+                post_v.append(lambda: stage_gq(ug))
+            if G_E and due(st, OFF_G - 2) is not None:
+                post_v.append(lambda: stage_f(2 * due(st, OFF_G - 2) + 1))
+            if uh is not None:
+                mxs += stage_h(st, uh)
+                if tail or uh % I_S_EVERY == I_S_EVERY - 1:
+                    post_s.append(lambda: stage_i(uh, "s"))
+                else:
+                    post_v.append(lambda: stage_i(uh, "v"))
+            if uj is not None:
+                ts += stage_j(st, uj)
+                if tail or G_K:
+                    post_s.append(lambda: stage_k(uj, "s"))
+                else:
+                    post_v.append(lambda: stage_k(uj, "v"))
+            if ul is not None:
+                post_v.append(lambda: stage_l(ul))
+            if G_K and due(st, OFF_L - 2) is not None:
+                post_v.append(lambda: stage_k2(due(st, OFF_L - 2)))
+            if um is not None:
+                mxs += stage_m(st, um)
+                post_v.append(lambda: stage_n(um))
+            weave(mms, ds, mxs, ts)
+            if st < UNITS:
+                stage_b(st)
+            for f in post_s:
+                f()
+            if st < UNITS:
+                stage_c(st)
+            for f in post_v:
+                f()

@@ -20,10 +20,10 @@ FLOPS = 2 * B * H * N * N * DH * 2 + 2 * B * N * H * DH * D
 UNITS = B * 8 * H
 PAIRS = UNITS // 2
 MANUAL = True
-G_E = False
+G_E = True
 G_K = False
-OFF_G, OFF_H, OFF_J, OFF_L, OFF_M = 4, 7, 10, 11, 13
-QK_V = 2
+OFF_G, OFF_H, OFF_J, OFF_L, OFF_M = 6, 9, 12, 13, 15
+QK_S_EVERY = 2
 I_S_EVERY = 4
 TAIL_S = True
 
@@ -407,7 +407,9 @@ def tile_mmattn_pb_t_kernel(tc, q_rot, k_rot, v, w_out1, b_out1, w_out2, b_out2,
                 x, h, a = GROUPS[gi]
                 trs, evac = qk_group(st, x, b, h, a)
                 ts += trs
-                if (st % 4 == QK_V) == (n % 2 == 0):
+                if st > 0 and (QK_S_EVERY == 0 or (st // 2 + n) % QK_S_EVERY != 0):
+                    post_v.append(lambda evac=evac: evac("v"))
+                elif st == 0 and n % 2 == 1:
                     post_v.append(lambda evac=evac: evac("v"))
                 else:
                     post_s.append(lambda evac=evac: evac("s"))

@@ -26,6 +26,7 @@ OFF_G, OFF_H, OFF_J, OFF_L, OFF_M = 6, 9, 12, 13, 15
 QK_S_EVERY = 2
 I_S_EVERY = 4
 TAIL_S = True
+GAP = 1
 
 
 def tile_mmattn_pb_t_kernel(tc, q_rot, k_rot, v, w_out1, b_out1, w_out2, b_out2, out_0, out_1):
@@ -198,6 +199,10 @@ def tile_mmattn_pb_t_kernel(tc, q_rot, k_rot, v, w_out1, b_out1, w_out2, b_out2,
             m2 = st4.tile([P, 2], F32, name="m2")
             for g in range(2):
                 nc.vector.reduce_max(out=m2[:, g:g + 1], in_=banks[g][:], axis=AX.X)
+            live[("m2", i)] = m2
+
+        def stage_b2(i):
+            m2 = live[("m2", i)]
             negmax = st4.tile([P, 1], F32, name="negmax")
             nc.vector.tensor_scalar(
                 out=negmax[:], in0=m2[:, 0:1], scalar1=m2[:, 1:2], scalar2=-SCALE, op0=ALU.max, op1=ALU.mult
@@ -252,16 +257,24 @@ def tile_mmattn_pb_t_kernel(tc, q_rot, k_rot, v, w_out1, b_out1, w_out2, b_out2,
             rs = live[("rs", u)]
             e_codes = gp.tile([P, 4 * P], U32, name="e_codes", align_bytes=64)
             e_scales = gp.tile([P, 4 * P], U8, name="e_scales", align_bytes=64)
-            for h in range(H):
-                nc.vector.quantize_mx(
+            rsum = st4.tile([P, 2], F32, name="rsum")
+            rinv = st4.tile([P, 2], F32, name="rinv")
+            live[("ec", u)] = (e_codes, e_scales, rinv)
+
+            def quant(h):
+                return lambda: nc.vector.quantize_mx(
                     out=e_codes[:, h * 256:(h + 1) * 256].bitcast(FP8X4), scales=e_scales[:, h * 256:(h + 1) * 256],
                     in_=live[("eg", 2 * u + h)][:].rearrange("p g q j -> p (g q j)"),
                 )
-            rsum = st4.tile([P, 2], F32, name="rsum")
-            nc.vector.tensor_reduce(out=rsum[:], in_=rs[:].rearrange("p (h g) -> p h g", g=2), axis=AX.X, op=ALU.add)
-            rinv = st4.tile([P, 2], F32, name="rinv")
-            nc.vector.reciprocal(out=rinv[:], in_=rsum[:])
-            live[("ec", u)] = (e_codes, e_scales, rinv)
+
+            return [
+                quant(0),
+                lambda: nc.vector.tensor_reduce(
+                    out=rsum[:], in_=rs[:].rearrange("p (h g) -> p h g", g=2), axis=AX.X, op=ALU.add
+                ),
+                quant(1),
+                lambda: nc.vector.reciprocal(out=rinv[:], in_=rsum[:]),
+            ]
 
         def stage_h(st, u):
             b = u // 8
@@ -289,16 +302,18 @@ def tile_mmattn_pb_t_kernel(tc, q_rot, k_rot, v, w_out1, b_out1, w_out2, b_out2,
             rinv = live[("ec", u)][2]
             attn = ap3.tile([P, H * DH], BF16, name="attn")
             live[("attn", u)] = attn
-            for h in range(H):
+
+            def scaled(h):
                 if eng == "v":
-                    nc.vector.tensor_scalar(
+                    return lambda: nc.vector.tensor_scalar(
                         out=attn[:, h * DH:(h + 1) * DH], in0=pv[:, h, :], scalar1=rinv[:, h:h + 1], scalar2=None,
                         op0=ALU.mult,
                     )
-                else:
-                    nc.scalar.activation(
-                        out=attn[:, h * DH:(h + 1) * DH], in_=pv[:, h, :], func=ACT.Copy, scale=rinv[:, h:h + 1]
-                    )
+                return lambda: nc.scalar.activation(
+                    out=attn[:, h * DH:(h + 1) * DH], in_=pv[:, h, :], func=ACT.Copy, scale=rinv[:, h:h + 1]
+                )
+
+            return [scaled(h) for h in range(H)]
 
         def stage_j(st, u):
             attn = live[("attn", u)]
@@ -415,15 +430,15 @@ def tile_mmattn_pb_t_kernel(tc, q_rot, k_rot, v, w_out1, b_out1, w_out2, b_out2,
                     post_s.append(lambda evac=evac: evac("s"))
             ug, uh, uj, ul, um = due(st, OFF_G), due(st, OFF_H), due(st, OFF_J), due(st, OFF_L), due(st, OFF_M)
             if ug is not None:
-                post_v.append(lambda: stage_gq(ug))
+                post_v += stage_gq(ug)
             if G_E and due(st, OFF_G - 2) is not None:
                 post_v.append(lambda: stage_f(2 * due(st, OFF_G - 2) + 1))
             if uh is not None:
                 mxs += stage_h(st, uh)
                 if tail or uh % I_S_EVERY == I_S_EVERY - 1:
-                    post_s.append(lambda: stage_i(uh, "s"))
+                    post_s += stage_i(uh, "s")
                 else:
-                    post_v.append(lambda: stage_i(uh, "v"))
+                    post_v += stage_i(uh, "v")
             if uj is not None:
                 ts += stage_j(st, uj)
                 if tail or G_K:
@@ -440,6 +455,10 @@ def tile_mmattn_pb_t_kernel(tc, q_rot, k_rot, v, w_out1, b_out1, w_out2, b_out2,
             weave(mms, ds, mxs, ts)
             if st < UNITS:
                 stage_b(st)
+                for f in post_v[:GAP]:
+                    f()
+                post_v = post_v[GAP:]
+                stage_b2(st)
             for f in post_s:
                 f()
             if st < UNITS:

@@ -21,12 +21,14 @@ UNITS = B * 8 * H
 PAIRS = UNITS // 2
 MANUAL = True
 G_E = True
-G_K = False
-OFF_G, OFF_H, OFF_J, OFF_L, OFF_M = 6, 9, 12, 13, 15
-QK_S_EVERY = 2
+G_K = True
+OFF_G, OFF_H, OFF_J, OFF_L, OFF_M = 6, 9, 12, 15, 17
+QK_S_EVERY = 0
 I_S_EVERY = 4
 TAIL_S = True
 GAP = 1
+G_TAIL = 1
+GK_TAIL = 3
 
 
 def tile_mmattn_pb_t_kernel(tc, q_rot, k_rot, v, w_out1, b_out1, w_out2, b_out2, out_0, out_1):
@@ -73,28 +75,28 @@ def tile_mmattn_pb_t_kernel(tc, q_rot, k_rot, v, w_out1, b_out1, w_out2, b_out2,
 
         def load_batch(b):
             for h in range(H):
-                load("k", b, h, (0, 1))
                 load("q", b, h, (0, 1))
+                load("k", b, h, (0, 1))
             for h in range(H):
                 load("v", b, h, (0, 1))
 
         for h in range(H):
+            load("q", 0, h, (0,))
             load("k", 0, h, (0,))
             load("k", 0, h, (1,))
-            load("q", 0, h, (0,))
         for h in range(H):
             load("v", 0, h, (0, 1))
-        load("k", 1, 0, (0, 1))
+        load("q", 1, 0, (0, 1))
         for h in range(H):
             load("q", 0, h, (1,))
-        load("q", 1, 0, (0, 1))
+        load("k", 1, 0, (0, 1))
         w_raw = consts.tile([P, 2, 4, D], BF16)
         bias_bf = consts.tile([P, 2, D], BF16)
         for s, (w, bb) in enumerate(((w_out1, b_out1), (w_out2, b_out2))):
             nc.sync.dma_start(out=w_raw[:, s], in_=w.rearrange("(j p) o -> p j o", p=P))
             nc.sync.dma_start(out=bias_bf[:, s, :], in_=bb.partition_broadcast(P))
-        load("k", 1, 1, (0, 1))
         load("q", 1, 1, (0, 1))
+        load("k", 1, 1, (0, 1))
         for h in range(H):
             load("v", 1, h, (0, 1))
 
@@ -120,7 +122,7 @@ def tile_mmattn_pb_t_kernel(tc, q_rot, k_rot, v, w_out1, b_out1, w_out2, b_out2,
                 nc.scalar.copy(out=out, in_=in_)
 
         def misc_bank(st, shape, dtype, name):
-            if st >= UNITS + 2:
+            if st < 0 or st >= UNITS + 2:
                 return ps_s.tile(shape, dtype, name=name, tag="s_ps")
             return ps_m.tile(shape, dtype, name=name, tag="m")
 
@@ -139,8 +141,8 @@ def tile_mmattn_pb_t_kernel(tc, q_rot, k_rot, v, w_out1, b_out1, w_out2, b_out2,
             ]
             return trs, lambda eng: copy_on(eng, dst[:, a * 512:(a + 1) * 512], bank[:].rearrange("p c t -> p (c t)"))
 
-        GROUPS = [("k", 0, 0), ("k", 0, 1), ("q", 0, 0), ("k", 1, 0), ("k", 1, 1), ("q", 1, 0), ("q", 0, 1), ("q", 1, 1)]
-        qk_plan = {0: [(0, 3), (0, 4), (0, 5)], 4: [(0, 6)], 6: [(0, 7)]}
+        GROUPS = [("q", 0, 0), ("k", 0, 0), ("k", 0, 1), ("q", 1, 0), ("k", 1, 0), ("k", 1, 1), ("q", 0, 1), ("q", 1, 1)]
+        qk_plan = {0: [(0, 4), (0, 5)], 4: [(0, 6)], 6: [(0, 7)]}
         for b in range(1, B):
             for n in range(8):
                 step = 16 * (b - 1) + 2 * n + 2
@@ -233,9 +235,12 @@ def tile_mmattn_pb_t_kernel(tc, q_rot, k_rot, v, w_out1, b_out1, w_out2, b_out2,
                 (lambda x=x: nc.tensor.transpose(et_ps[:, x, :], e_sb[:, x, :], ident_b[:])) for x in range(8)
             ]
 
+        def via_gpsimd(i):
+            return G_E and i % 2 == 1 and i < UNITS - 2 * G_TAIL
+
         def stage_e(i, eng):
             et_ps = live[("et", i)]
-            if G_E and i % 2 == 1:
+            if via_gpsimd(i):
                 et_raw = gp.tile([P, 8, P], BF16, name="et_raw")
                 copy_on(eng, et_raw[:], et_ps[:])
                 live[("etr", i)] = et_raw
@@ -324,9 +329,12 @@ def tile_mmattn_pb_t_kernel(tc, q_rot, k_rot, v, w_out1, b_out1, w_out2, b_out2,
                 for j in range(4)
             ]
 
+        def k_via_gpsimd(u):
+            return G_K and u < PAIRS - GK_TAIL
+
         def stage_k(u, eng):
             at_ps = live[("at", u)]
-            if G_K:
+            if k_via_gpsimd(u):
                 at_raw = ap3.tile([P, 4, P], BF16, name="at_raw")
                 copy_on(eng, at_raw[:], at_ps[:])
                 live[("atr", u)] = at_raw
@@ -390,9 +398,9 @@ def tile_mmattn_pb_t_kernel(tc, q_rot, k_rot, v, w_out1, b_out1, w_out2, b_out2,
                 return (st - off) // 2
             return None
 
-        for n in range(3):
+        for n in range(4):
             x, h, a = GROUPS[n]
-            trs, evac = qk_group(0, x, 0, h, a)
+            trs, evac = qk_group(-1, x, 0, h, a)
             for f in trs:
                 f()
             evac("v" if n % 2 == 0 else "s")
@@ -424,15 +432,14 @@ def tile_mmattn_pb_t_kernel(tc, q_rot, k_rot, v, w_out1, b_out1, w_out2, b_out2,
                 ts += trs
                 if st > 0 and (QK_S_EVERY == 0 or (st // 2 + n) % QK_S_EVERY != 0):
                     post_v.append(lambda evac=evac: evac("v"))
-                elif st == 0 and n % 2 == 1:
-                    post_v.append(lambda evac=evac: evac("v"))
                 else:
                     post_s.append(lambda evac=evac: evac("s"))
             ug, uh, uj, ul, um = due(st, OFF_G), due(st, OFF_H), due(st, OFF_J), due(st, OFF_L), due(st, OFF_M)
             if ug is not None:
                 post_v += stage_gq(ug)
-            if G_E and due(st, OFF_G - 2) is not None:
-                post_v.append(lambda: stage_f(2 * due(st, OFF_G - 2) + 1))
+            uf = due(st, OFF_G - 2)
+            if uf is not None and via_gpsimd(2 * uf + 1):
+                post_v.append(lambda: stage_f(2 * uf + 1))
             if uh is not None:
                 mxs += stage_h(st, uh)
                 if tail or uh % I_S_EVERY == I_S_EVERY - 1:
@@ -441,14 +448,15 @@ def tile_mmattn_pb_t_kernel(tc, q_rot, k_rot, v, w_out1, b_out1, w_out2, b_out2,
                     post_v += stage_i(uh, "v")
             if uj is not None:
                 ts += stage_j(st, uj)
-                if tail or G_K:
+                if tail or k_via_gpsimd(uj):
                     post_s.append(lambda: stage_k(uj, "s"))
                 else:
                     post_v.append(lambda: stage_k(uj, "v"))
             if ul is not None:
                 post_v.append(lambda: stage_l(ul))
-            if G_K and due(st, OFF_L - 2) is not None:
-                post_v.append(lambda: stage_k2(due(st, OFF_L - 2)))
+            uk = due(st, OFF_L - 2)
+            if uk is not None and k_via_gpsimd(uk):
+                post_v.append(lambda: stage_k2(uk))
             if um is not None:
                 mxs += stage_m(st, um)
                 post_v.append(lambda: stage_n(um))

@@ -24,9 +24,10 @@ G_E = True
 G_K = True
 OFF_G, OFF_H, OFF_J, OFF_L, OFF_M = 6, 9, 12, 15, 17
 QK_S_EVERY = 0
-I_S_EVERY = 4
+I_S_EVERY = 1000
 TAIL_S = True
 GAP = 1
+TS_EARLY = False
 G_TAIL = 1
 GK_TAIL = 3
 
@@ -385,12 +386,24 @@ def tile_mmattn_pb_t_kernel(tc, q_rot, k_rot, v, w_out1, b_out1, w_out2, b_out2,
         def weave(mms, ds, mxs, ts):
             per = 3
             pos = 0
-            for mm in mms:
+            if not mms or not TS_EARLY:
+                for mm in mms:
+                    mm()
+                    for f in ds[pos:pos + per]:
+                        f()
+                    pos += per
+                for f in ds[pos:] + mxs + ts:
+                    f()
+                return
+            for mm in mms[:3]:
                 mm()
                 for f in ds[pos:pos + per]:
                     f()
                 pos += per
-            for f in ds[pos:] + mxs + ts:
+            for f in ds[pos:] + ts:
+                f()
+            mms[3]()
+            for f in mxs:
                 f()
 
         def due(st, off):

@@ -20,16 +20,12 @@ FLOPS = 2 * B * H * N * N * DH * 2 + 2 * B * N * H * DH * D
 UNITS = B * 8 * H
 PAIRS = UNITS // 2
 MANUAL = True
-G_E = True
-G_K = True
 OFF_G, OFF_H, OFF_J, OFF_L, OFF_M = 6, 9, 12, 15, 17
 QK_S_EVERY = 0
 I_S_EVERY = 1000
 TAIL_S = True
 GAP = 1
 TS_EARLY = False
-G_TAIL = 1
-GK_TAIL = 3
 
 
 def tile_mmattn_pb_t_kernel(tc, q_rot, k_rot, v, w_out1, b_out1, w_out2, b_out2, out_0, out_1):
@@ -43,7 +39,6 @@ def tile_mmattn_pb_t_kernel(tc, q_rot, k_rot, v, w_out1, b_out1, w_out2, b_out2,
         vq = ctx.enter_context(tc.tile_pool(name="vq", bufs=2))
         ep = ctx.enter_context(tc.tile_pool(name="ep", bufs=4))
         gp = ctx.enter_context(tc.tile_pool(name="gp", bufs=3))
-        g1 = ctx.enter_context(tc.tile_pool(name="g1", bufs=1))
         st4 = ctx.enter_context(tc.tile_pool(name="st4", bufs=6))
         ap3 = ctx.enter_context(tc.tile_pool(name="ap3", bufs=3))
         ps_s = ctx.enter_context(tc.psum_pool(name="ps_s", bufs=4))
@@ -54,8 +49,6 @@ def tile_mmattn_pb_t_kernel(tc, q_rot, k_rot, v, w_out1, b_out1, w_out2, b_out2,
 
         ident_f = consts.tile([P, P], F32)
         make_identity(nc, ident_f[:])
-        ident_b = consts.tile([P, P], BF16)
-        make_identity(nc, ident_b[:])
 
         raws = {}
 
@@ -94,7 +87,7 @@ def tile_mmattn_pb_t_kernel(tc, q_rot, k_rot, v, w_out1, b_out1, w_out2, b_out2,
         w_raw = consts.tile([P, 2, 4, D], BF16)
         bias_bf = consts.tile([P, 2, D], BF16)
         for s, (w, bb) in enumerate(((w_out1, b_out1), (w_out2, b_out2))):
-            nc.sync.dma_start(out=w_raw[:, s], in_=w.rearrange("(j p) o -> p j o", p=P))
+            nc.sync.dma_start(out=w_raw[:, s], in_=w.rearrange("(p j) o -> p j o", j=4))
             nc.sync.dma_start(out=bias_bf[:, s, :], in_=bb.partition_broadcast(P))
         load("q", 1, 1, (0, 1))
         load("k", 1, 1, (0, 1))
@@ -140,7 +133,12 @@ def tile_mmattn_pb_t_kernel(tc, q_rot, k_rot, v, w_out1, b_out1, w_out2, b_out2,
                 (lambda c=c: nc.tensor.transpose(bank[:, c, :], src[:, a, c, :].bitcast(F32), ident_f[:]))
                 for c in range(4)
             ]
-            return trs, lambda eng: copy_on(eng, dst[:, a * 512:(a + 1) * 512], bank[:].rearrange("p c t -> p (c t)"))
+            out = dst[:, a * 512:(a + 1) * 512]
+            if x == "q":
+                return trs, lambda eng: copy_on(eng, out, bank[:].rearrange("p c t -> p (c t)"))
+            return trs, lambda eng: copy_on(
+                eng, out.rearrange("p (u t e) -> p u t e", u=2, e=2), bank[:].rearrange("p (u e) t -> p u t e", e=2)
+            )
 
         GROUPS = [("q", 0, 0), ("k", 0, 0), ("k", 0, 1), ("q", 1, 0), ("k", 1, 0), ("k", 1, 1), ("q", 0, 1), ("q", 1, 1)]
         qk_plan = {0: [(0, 4), (0, 5)], 4: [(0, 6)], 6: [(0, 7)]}
@@ -159,10 +157,12 @@ def tile_mmattn_pb_t_kernel(tc, q_rot, k_rot, v, w_out1, b_out1, w_out2, b_out2,
                 v_grp = vq.tile([P, 2, DH, 4], BF16, name="v_grp%d" % h, align_bytes=64)
                 vcs[("g", b, h)] = v_grp
             v_grp = vcs[("g", b, h)]
-            nc.gpsimd.tensor_scalar(
-                out=v_grp[:, g], in0=raws[("v", b, h)][:, g].rearrange("p j d -> p d j"),
-                scalar1=1.0, scalar2=0.0, op0=ALU.mult, op1=ALU.add,
-            )
+            dst = v_grp[:, g].rearrange("p (u x e) j -> p u x e j", u=2, e=2)
+            src = raws[("v", b, h)][:, g].rearrange("p j (x u e) -> p u x e j", u=2, e=2)
+            for u in range(2):
+                nc.gpsimd.tensor_scalar(
+                    out=dst[:, u], in0=src[:, u], scalar1=1.0, scalar2=0.0, op0=ALU.mult, op1=ALU.add,
+                )
 
         def v_quant(b, h):
             v_codes = vq.tile([P, 2 * DH], U32, name="v_codes%d" % h, align_bytes=64)
@@ -230,33 +230,17 @@ def tile_mmattn_pb_t_kernel(tc, q_rot, k_rot, v, w_out1, b_out1, w_out2, b_out2,
 
         def stage_d(i):
             e_sb = live[("e", i)]
-            et_ps = ps_t.tile([P, 8, P], BF16, name="et_ps")
+            et_ps = ps_t.tile([P, 4, P], F32, name="et_ps")
             live[("et", i)] = et_ps
+            words = e_sb[:].rearrange("p j m -> p (j m)").bitcast(F32)
             return [
-                (lambda x=x: nc.tensor.transpose(et_ps[:, x, :], e_sb[:, x, :], ident_b[:])) for x in range(8)
+                (lambda x=x: nc.tensor.transpose(et_ps[:, x, :], words[:, x * P:(x + 1) * P], ident_f[:])) for x in range(4)
             ]
-
-        def via_gpsimd(i):
-            return G_E and i % 2 == 1 and i < UNITS - 2 * G_TAIL
 
         def stage_e(i, eng):
             et_ps = live[("et", i)]
-            if via_gpsimd(i):
-                et_raw = gp.tile([P, 8, P], BF16, name="et_raw")
-                copy_on(eng, et_raw[:], et_ps[:])
-                live[("etr", i)] = et_raw
-            else:
-                eg = gp.tile([P, 2, P, 4], BF16, name="eg%d" % (i % 2), align_bytes=64)
-                copy_on(eng, eg[:], et_ps[:].rearrange("p (g j) q -> p g q j", j=4))
-                live[("eg", i)] = eg
-
-        def stage_f(i):
-            et_raw = live[("etr", i)]
-            eg = g1.tile([P, 2, P, 4], BF16, name="eg_g", align_bytes=64)
-            nc.gpsimd.tensor_scalar(
-                out=eg[:], in0=et_raw[:].rearrange("p (g j) q -> p g q j", j=4),
-                scalar1=1.0, scalar2=0.0, op0=ALU.mult, op1=ALU.add,
-            )
+            eg = gp.tile([P, 2, P, 2], F32, name="eg%d" % (i % 2), align_bytes=64)
+            copy_on(eng, eg[:], et_ps[:].rearrange("p (g u) q -> p g q u", u=2))
             live[("eg", i)] = eg
 
         def stage_gq(u):
@@ -270,7 +254,7 @@ def tile_mmattn_pb_t_kernel(tc, q_rot, k_rot, v, w_out1, b_out1, w_out2, b_out2,
             def quant(h):
                 return lambda: nc.vector.quantize_mx(
                     out=e_codes[:, h * 256:(h + 1) * 256].bitcast(FP8X4), scales=e_scales[:, h * 256:(h + 1) * 256],
-                    in_=live[("eg", 2 * u + h)][:].rearrange("p g q j -> p (g q j)"),
+                    in_=live[("eg", 2 * u + h)][:].rearrange("p g q u -> p (g q u)").bitcast(BF16),
                 )
 
             return [
@@ -310,46 +294,30 @@ def tile_mmattn_pb_t_kernel(tc, q_rot, k_rot, v, w_out1, b_out1, w_out2, b_out2,
             live[("attn", u)] = attn
 
             def scaled(h):
+                dst = attn[:].rearrange("p (u h x) -> p u h x", u=2, h=H)[:, :, h, :]
+                src = pv[:, h, :].rearrange("p (u x) -> p u x", u=2)
                 if eng == "v":
                     return lambda: nc.vector.tensor_scalar(
-                        out=attn[:, h * DH:(h + 1) * DH], in0=pv[:, h, :], scalar1=rinv[:, h:h + 1], scalar2=None,
-                        op0=ALU.mult,
+                        out=dst, in0=src, scalar1=rinv[:, h:h + 1], scalar2=None, op0=ALU.mult,
                     )
-                return lambda: nc.scalar.activation(
-                    out=attn[:, h * DH:(h + 1) * DH], in_=pv[:, h, :], func=ACT.Copy, scale=rinv[:, h:h + 1]
-                )
+                return lambda: nc.scalar.activation(out=dst, in_=src, func=ACT.Copy, scale=rinv[:, h:h + 1])
 
             return [scaled(h) for h in range(H)]
 
         def stage_j(st, u):
             attn = live[("attn", u)]
-            at_ps = misc_bank(st, [P, 4, P], BF16, "at_ps")
+            at_ps = misc_bank(st, [P, 2, P], F32, "at_ps")
             live[("at", u)] = at_ps
+            words = attn[:].bitcast(F32)
             return [
-                (lambda j=j: nc.tensor.transpose(at_ps[:, j, :], attn[:, j * P:(j + 1) * P], ident_b[:]))
-                for j in range(4)
+                (lambda x=x: nc.tensor.transpose(at_ps[:, x, :], words[:, x * P:(x + 1) * P], ident_f[:]))
+                for x in range(2)
             ]
-
-        def k_via_gpsimd(u):
-            return G_K and u < PAIRS - GK_TAIL
 
         def stage_k(u, eng):
             at_ps = live[("at", u)]
-            if k_via_gpsimd(u):
-                at_raw = ap3.tile([P, 4, P], BF16, name="at_raw")
-                copy_on(eng, at_raw[:], at_ps[:])
-                live[("atr", u)] = at_raw
-            else:
-                ag = ap3.tile([P, P, 4], BF16, name="ag", align_bytes=64)
-                copy_on(eng, ag[:], at_ps[:].rearrange("p j q -> p q j"))
-                live[("ag", u)] = ag
-
-        def stage_k2(u):
-            at_raw = live[("atr", u)]
-            ag = g1.tile([P, P, 4], BF16, name="ag_g", align_bytes=64)
-            nc.gpsimd.tensor_scalar(
-                out=ag[:], in0=at_raw[:].rearrange("p j q -> p q j"), scalar1=1.0, scalar2=0.0, op0=ALU.mult, op1=ALU.add
-            )
+            ag = ap3.tile([P, P, 2], F32, name="ag", align_bytes=64)
+            copy_on(eng, ag[:], at_ps[:].rearrange("p u q -> p q u"))
             live[("ag", u)] = ag
 
         def stage_l(u):
@@ -357,7 +325,7 @@ def tile_mmattn_pb_t_kernel(tc, q_rot, k_rot, v, w_out1, b_out1, w_out2, b_out2,
             a_codes = ap3.tile([P, P], U32, name="a_codes", align_bytes=64)
             a_scales = ap3.tile([P, P], U8, name="a_scales", align_bytes=64)
             nc.vector.quantize_mx(
-                out=a_codes[:].bitcast(FP8X4), scales=a_scales[:], in_=ag[:].rearrange("p q j -> p (q j)")
+                out=a_codes[:].bitcast(FP8X4), scales=a_scales[:], in_=ag[:].rearrange("p q u -> p (q u)").bitcast(BF16)
             )
             live[("ac", u)] = (a_codes, a_scales)
 
@@ -450,9 +418,6 @@ def tile_mmattn_pb_t_kernel(tc, q_rot, k_rot, v, w_out1, b_out1, w_out2, b_out2,
             ug, uh, uj, ul, um = due(st, OFF_G), due(st, OFF_H), due(st, OFF_J), due(st, OFF_L), due(st, OFF_M)
             if ug is not None:
                 post_v += stage_gq(ug)
-            uf = due(st, OFF_G - 2)
-            if uf is not None and via_gpsimd(2 * uf + 1):
-                post_v.append(lambda: stage_f(2 * uf + 1))
             if uh is not None:
                 mxs += stage_h(st, uh)
                 if tail or uh % I_S_EVERY == I_S_EVERY - 1:
@@ -461,15 +426,9 @@ def tile_mmattn_pb_t_kernel(tc, q_rot, k_rot, v, w_out1, b_out1, w_out2, b_out2,
                     post_v += stage_i(uh, "v")
             if uj is not None:
                 ts += stage_j(st, uj)
-                if tail or k_via_gpsimd(uj):
-                    post_s.append(lambda: stage_k(uj, "s"))
-                else:
-                    post_v.append(lambda: stage_k(uj, "v"))
+                post_s.append(lambda: stage_k(uj, "s"))
             if ul is not None:
                 post_v.append(lambda: stage_l(ul))
-            uk = due(st, OFF_L - 2)
-            if uk is not None and k_via_gpsimd(uk):
-                post_v.append(lambda: stage_k2(uk))
             if um is not None:
                 mxs += stage_m(st, um)
                 post_v.append(lambda: stage_n(um))

@@ -22,7 +22,6 @@ PAIRS = UNITS // 2
 MANUAL = True
 OFF_G, OFF_H, OFF_J, OFF_L, OFF_M = 6, 9, 12, 15, 17
 QK_S_EVERY = 0
-I_S_EVERY = 1000
 TAIL_S = True
 GAP = 1
 TS_EARLY = False
@@ -420,10 +419,7 @@ def tile_mmattn_pb_t_kernel(tc, q_rot, k_rot, v, w_out1, b_out1, w_out2, b_out2,
                 post_v += stage_gq(ug)
             if uh is not None:
                 mxs += stage_h(st, uh)
-                if tail or uh % I_S_EVERY == I_S_EVERY - 1:
-                    post_s += stage_i(uh, "s")
-                else:
-                    post_v += stage_i(uh, "v")
+                post_s += stage_i(uh, "s")
             if uj is not None:
                 ts += stage_j(st, uj)
                 post_s.append(lambda: stage_k(uj, "s"))

@@ -19,12 +19,48 @@ FLOPS = 2 * B * H * N * N * DH * 2 + 2 * B * N * H * DH * D
 
 UNITS = B * 8 * H
 PAIRS = UNITS // 2
-MANUAL = True
-OFF_G, OFF_H, OFF_J, OFF_L, OFF_M = 6, 9, 12, 15, 17
-QK_S_EVERY = 0
-TAIL_S = True
-GAP = 1
-TS_EARLY = False
+OFF_G, OFF_R, OFF_H, OFF_I, OFF_J, OFF_K, OFF_L, OFF_M, OFF_N = 4, 5, 6, 7, 10, 10, 10, 11, 11
+OFF_D, OFF_E = 2, 2
+QK_PAR = 3
+BANKS = {"s": ("s", 4), "et": ("et", 1), "pv": ("pv", 1), "qk": ("qk", 1), "at": ("ao", 1), "o": ("ao", 1)}
+PE_ORDER = ["a0", "a1", "D", "Q", "J", "a2", "a3", "H", "M"]
+V_ORDER = ["L", "N", "G", "Q"]
+S_ORDER = ["E", "I", "K", "C"]
+FILL = ["sum", "recip"]
+I_ENG = ("s", "s")
+K_ENG = "s"
+Q_ENG = "v"
+E_ENG = ("s", "s")
+SWAP = True
+PW = (6, 6)
+PW_ENG = "g"
+TAIL_I = ("s", "v")
+TAIL_K = "s"
+EARLY_Q = 0
+LOADS = 0
+LATE_KIND = "at"
+
+BANKS = {"s": ("s", 4,), "et": ("et", 1,), "pv": ("pv", 1,), "qk": ("x", 2,), "at": ("x", 2,), "o": ("x", 2,)}
+OFF_G = 4
+OFF_R = 5
+OFF_H = 6
+OFF_I = 6
+OFF_J = 9
+OFF_K = 9
+OFF_L = 12
+OFF_M = 16
+OFF_N = 16
+QK_PAR = 3
+PE_ORDER = ("a0", "a1", "a2", "a3", "D", "Q", "J", "H", "M",)
+V_ORDER = ("G", "L", "I", "Q", "N",)
+S_ORDER = ("E", "I", "K", "C",)
+EARLY_Q = 1
+TAIL_I = ("s", "s",)
+SWAP = True
+PW = (6, 10,)
+PW_ENG = "g"
+I_ENG = ("s", "s",)
+Q_ENG = "v"
 
 
 def tile_mmattn_pb_t_kernel(tc, q_rot, k_rot, v, w_out1, b_out1, w_out2, b_out2, out_0, out_1):
@@ -40,11 +76,11 @@ def tile_mmattn_pb_t_kernel(tc, q_rot, k_rot, v, w_out1, b_out1, w_out2, b_out2,
         gp = ctx.enter_context(tc.tile_pool(name="gp", bufs=3))
         st4 = ctx.enter_context(tc.tile_pool(name="st4", bufs=6))
         ap3 = ctx.enter_context(tc.tile_pool(name="ap3", bufs=3))
-        ps_s = ctx.enter_context(tc.psum_pool(name="ps_s", bufs=4))
-        ps_t = ctx.enter_context(tc.psum_pool(name="ps_t", bufs=2))
-        ps_m = ctx.enter_context(tc.psum_pool(name="ps_m", bufs=2))
-        if MANUAL:
-            ctx.enter_context(tc.manual_schedule())
+        ps = {}
+        for kind, (nm, nb) in BANKS.items():
+            if nm not in ps:
+                ps[nm] = ctx.enter_context(tc.psum_pool(name="ps_" + nm, bufs=nb))
+        ctx.enter_context(tc.manual_schedule())
 
         ident_f = consts.tile([P, P], F32)
         make_identity(nc, ident_f[:])
@@ -73,10 +109,18 @@ def tile_mmattn_pb_t_kernel(tc, q_rot, k_rot, v, w_out1, b_out1, w_out2, b_out2,
             for h in range(H):
                 load("v", b, h, (0, 1))
 
-        for h in range(H):
-            load("q", 0, h, (0,))
-            load("k", 0, h, (0,))
-            load("k", 0, h, (1,))
+        if LOADS == 0:
+            for h in range(H):
+                load("q", 0, h, (0,))
+                load("k", 0, h, (0,))
+                load("k", 0, h, (1,))
+        else:
+            load("k", 0, 0, (0,))
+            load("q", 0, 0, (0,))
+            load("k", 0, 0, (1,))
+            load("k", 0, 1, (0,))
+            load("k", 0, 1, (1,))
+            load("q", 0, 1, (0,))
         for h in range(H):
             load("v", 0, h, (0, 1))
         load("q", 1, 0, (0, 1))
@@ -98,14 +142,21 @@ def tile_mmattn_pb_t_kernel(tc, q_rot, k_rot, v, w_out1, b_out1, w_out2, b_out2,
         w_scales = consts.tile([P, 2, D], U8, align_bytes=64)
         bias_f = consts.tile([P, 2, D], F32)
 
-        def prep_w():
-            for s in range(2):
-                nc.vector.tensor_copy(out=w_grp[:, s], in_=w_raw[:, s].rearrange("p j o -> p o j"))
-            nc.vector.tensor_copy(out=bias_f[:], in_=bias_bf[:])
+        def prep_w0(s):
+            src = w_raw[:, s].rearrange("p j o -> p o j")
+            if PW_ENG == "g":
+                nc.gpsimd.tensor_scalar(out=w_grp[:, s], in0=src, scalar1=1.0, scalar2=0.0, op0=ALU.mult, op1=ALU.add)
+                nc.gpsimd.tensor_scalar(
+                    out=bias_f[:, s], in0=bias_bf[:, s], scalar1=1.0, scalar2=0.0, op0=ALU.mult, op1=ALU.add
+                )
+            else:
+                nc.vector.tensor_copy(out=w_grp[:, s], in_=src)
+                nc.vector.tensor_copy(out=bias_f[:, s], in_=bias_bf[:, s])
+
+        def prep_w(s):
             nc.vector.quantize_mx(
-                out=w_codes[:].rearrange("p s o -> p (s o)").bitcast(FP8X4),
-                scales=w_scales[:].rearrange("p s o -> p (s o)"),
-                in_=w_grp[:].rearrange("p s o j -> p (s o j)"),
+                out=w_codes[:, s].bitcast(FP8X4), scales=w_scales[:, s],
+                in_=w_grp[:, s].rearrange("p o j -> p (o j)"),
             )
 
         def copy_on(eng, out, in_):
@@ -114,20 +165,22 @@ def tile_mmattn_pb_t_kernel(tc, q_rot, k_rot, v, w_out1, b_out1, w_out2, b_out2,
             else:
                 nc.scalar.copy(out=out, in_=in_)
 
-        def misc_bank(st, shape, dtype, name):
+
+        def misc_bank(st, kind, shape, dtype, name):
             if st < 0 or st >= UNITS + 2:
-                return ps_s.tile(shape, dtype, name=name, tag="s_ps")
-            return ps_m.tile(shape, dtype, name=name, tag="m")
+                kind = "s"
+            nm = BANKS[kind][0]
+            return ps[nm].tile(shape, dtype, name=name, tag=nm)
 
         xts = {}
 
-        def qk_group(st, x, b, h, a):
+        def qk_group(st, kind, x, b, h, a):
             src = raws[(x, b, h)]
             if (x, b, h) not in xts:
                 t = xt.tile([P, 8 * P], F32, name="xt_%s%d" % (x, h))
                 xts[(x, b, h)] = t
             dst = xts[(x, b, h)]
-            bank = misc_bank(st, [P, 4, P], F32, "bank_x")
+            bank = misc_bank(st, kind, [P, 4, P], F32, "bank_x")
             trs = [
                 (lambda c=c: nc.tensor.transpose(bank[:, c, :], src[:, a, c, :].bitcast(F32), ident_f[:]))
                 for c in range(4)
@@ -140,11 +193,13 @@ def tile_mmattn_pb_t_kernel(tc, q_rot, k_rot, v, w_out1, b_out1, w_out2, b_out2,
             )
 
         GROUPS = [("q", 0, 0), ("k", 0, 0), ("k", 0, 1), ("q", 1, 0), ("k", 1, 0), ("k", 1, 1), ("q", 0, 1), ("q", 1, 1)]
-        qk_plan = {0: [(0, 4), (0, 5)], 4: [(0, 6)], 6: [(0, 7)]}
+        qk_plan = {0: [(0, 4, "qk"), (0, 5, "pv")], 3: [(0, 6, "qk")], 5: [(0, 7, "qk")]}
         for b in range(1, B):
             for n in range(8):
-                step = 16 * (b - 1) + 2 * n + 2
-                qk_plan[step] = qk_plan.get(step, []) + [(b, n)]
+                qk_plan.setdefault(16 * (b - 1) + 2 * n + QK_PAR, []).append((b, n, "qk"))
+        for late in (3, 5):
+            if len(qk_plan[late]) > 1:
+                qk_plan[late][1] = qk_plan[late][1][:2] + (LATE_KIND,)
 
         def half(view, e):
             return view.bitcast(BF16).rearrange("p (x e) -> p x e", e=2)[:, :, e]
@@ -174,15 +229,24 @@ def tile_mmattn_pb_t_kernel(tc, q_rot, k_rot, v, w_out1, b_out1, w_out2, b_out2,
 
         live = {}
 
-        def stage_a(i):
+        def unit(i):
+            if SWAP and i in (1, 2):
+                i = 3 - i
             b, r = divmod(i, 16)
-            t, h = divmod(r, 2)
+            return b, r // 2, r % 2
+
+        def pair_of(i):
+            b, t, h = unit(i)
+            return 8 * b + t, h
+
+        def stage_a(i):
+            b, t, h = unit(i)
             qt = xts[("q", b, h)]
             kt = xts[("k", b, h)]
             banks = []
             mms = []
             for g in range(2):
-                s_ps = ps_s.tile([P, 512], F32, name="s_ps")
+                s_ps = ps["s"].tile([P, 512], F32, name="s_ps", tag="s")
                 banks.append(s_ps)
                 for e in range(2):
                     mms.append(
@@ -214,61 +278,59 @@ def tile_mmattn_pb_t_kernel(tc, q_rot, k_rot, v, w_out1, b_out1, w_out2, b_out2,
         def stage_c(i):
             banks = live[("s", i)]
             negmax = live[("negmax", i)]
-            if i % 2 == 0:
+            u, h = pair_of(i)
+            if h == 0:
                 rs = st4.tile([P, 4], F32, name="rs")
-                live[("rs", i // 2)] = rs
-            rs = live[("rs", i // 2)]
-            e_sb = ep.tile([P, 8, P], BF16, name="e_sb")
+                live[("rs", u)] = rs
+            rs = live[("rs", u)]
+            e_sb = ep.tile([P, 2, 512], BF16, name="e_sb")
             for g in range(2):
-                col = (i % 2) * 2 + g
+                col = h * 2 + g
                 nc.scalar.activation(
-                    out=e_sb[:, 4 * g:4 * g + 4, :].rearrange("p j m -> p (j m)"), in_=banks[g][:], func=ACT.Exp,
+                    out=e_sb[:, g, :], in_=banks[g][:], func=ACT.Exp,
                     bias=negmax[:, 0:1], scale=SCALE, accum_out=rs[:, col:col + 1],
                 )
             live[("e", i)] = e_sb
 
         def stage_d(i):
-            e_sb = live[("e", i)]
-            et_ps = ps_t.tile([P, 4, P], F32, name="et_ps")
+            words = live[("e", i)][:].rearrange("p g m -> p (g m)").bitcast(F32)
+            et_ps = misc_bank(0, "et", [P, 4, P], F32, "et_ps")
             live[("et", i)] = et_ps
-            words = e_sb[:].rearrange("p j m -> p (j m)").bitcast(F32)
             return [
                 (lambda x=x: nc.tensor.transpose(et_ps[:, x, :], words[:, x * P:(x + 1) * P], ident_f[:])) for x in range(4)
             ]
 
         def stage_e(i, eng):
             et_ps = live[("et", i)]
-            eg = gp.tile([P, 2, P, 2], F32, name="eg%d" % (i % 2), align_bytes=64)
+            eg = gp.tile([P, 2, P, 2], F32, name="eg%d" % pair_of(i)[1], align_bytes=64)
             copy_on(eng, eg[:], et_ps[:].rearrange("p (g u) q -> p g q u", u=2))
-            live[("eg", i)] = eg
+            live[("eg",) + pair_of(i)] = eg
 
-        def stage_gq(u):
+        def stage_sum(u):
             rs = live[("rs", u)]
+            rsum = st4.tile([P, 2], F32, name="rsum")
+            live[("rsum", u)] = rsum
+            nc.vector.tensor_reduce(out=rsum[:], in_=rs[:].rearrange("p (h g) -> p h g", g=2), axis=AX.X, op=ALU.add)
+
+        def stage_recip(u):
+            rinv = st4.tile([P, 2], F32, name="rinv")
+            live[("rinv", u)] = rinv
+            nc.vector.reciprocal(out=rinv[:], in_=live[("rsum", u)][:])
+
+        def stage_g(u):
             e_codes = gp.tile([P, 4 * P], U32, name="e_codes", align_bytes=64)
             e_scales = gp.tile([P, 4 * P], U8, name="e_scales", align_bytes=64)
-            rsum = st4.tile([P, 2], F32, name="rsum")
-            rinv = st4.tile([P, 2], F32, name="rinv")
-            live[("ec", u)] = (e_codes, e_scales, rinv)
-
-            def quant(h):
-                return lambda: nc.vector.quantize_mx(
+            live[("ec", u)] = (e_codes, e_scales)
+            for h in range(H):
+                nc.vector.quantize_mx(
                     out=e_codes[:, h * 256:(h + 1) * 256].bitcast(FP8X4), scales=e_scales[:, h * 256:(h + 1) * 256],
-                    in_=live[("eg", 2 * u + h)][:].rearrange("p g q u -> p (g q u)").bitcast(BF16),
+                    in_=live[("eg", u, h)][:].rearrange("p g q u -> p (g q u)").bitcast(BF16),
                 )
-
-            return [
-                quant(0),
-                lambda: nc.vector.tensor_reduce(
-                    out=rsum[:], in_=rs[:].rearrange("p (h g) -> p h g", g=2), axis=AX.X, op=ALU.add
-                ),
-                quant(1),
-                lambda: nc.vector.reciprocal(out=rinv[:], in_=rsum[:]),
-            ]
 
         def stage_h(st, u):
             b = u // 8
-            e_codes, e_scales, rinv = live[("ec", u)]
-            pv = misc_bank(st, [P, 2, DH], F32, "pv")
+            e_codes, e_scales = live[("ec", u)]
+            pv = misc_bank(st, "pv", [P, 2, DH], F32, "pv")
             live[("pv", u)] = pv
             mx = []
             for h in range(H):
@@ -286,37 +348,38 @@ def tile_mmattn_pb_t_kernel(tc, q_rot, k_rot, v, w_out1, b_out1, w_out2, b_out2,
                     )
             return mx
 
-        def stage_i(u, eng):
+        def stage_i(u):
             pv = live[("pv", u)]
-            rinv = live[("ec", u)][2]
+            rinv = live[("rinv", u)]
             attn = ap3.tile([P, H * DH], BF16, name="attn")
             live[("attn", u)] = attn
-
-            def scaled(h):
-                dst = attn[:].rearrange("p (u h x) -> p u h x", u=2, h=H)[:, :, h, :]
-                src = pv[:, h, :].rearrange("p (u x) -> p u x", u=2)
-                if eng == "v":
-                    return lambda: nc.vector.tensor_scalar(
-                        out=dst, in0=src, scalar1=rinv[:, h:h + 1], scalar2=None, op0=ALU.mult,
+            dst = attn[:].rearrange("p (u h x) -> p u h x", u=2, h=H)
+            def go(h, eng):
+                if eng == "s":
+                    nc.scalar.activation(
+                        out=dst[:, :, h, :], in_=pv[:, h, :].rearrange("p (u x) -> p u x", u=2), func=ACT.Copy,
+                        scale=rinv[:, h:h + 1],
                     )
-                return lambda: nc.scalar.activation(out=dst, in_=src, func=ACT.Copy, scale=rinv[:, h:h + 1])
-
-            return [scaled(h) for h in range(H)]
+                else:
+                    nc.vector.tensor_scalar(
+                        out=dst[:, :, h, :], in0=pv[:, h, :].rearrange("p (u x) -> p u x", u=2),
+                        scalar1=rinv[:, h:h + 1], scalar2=None, op0=ALU.mult,
+                    )
+            return go
 
         def stage_j(st, u):
-            attn = live[("attn", u)]
-            at_ps = misc_bank(st, [P, 2, P], F32, "at_ps")
+            words = live[("attn", u)][:].bitcast(F32)
+            at_ps = misc_bank(st, "at", [P, 2, P], F32, "at_ps")
             live[("at", u)] = at_ps
-            words = attn[:].bitcast(F32)
             return [
                 (lambda x=x: nc.tensor.transpose(at_ps[:, x, :], words[:, x * P:(x + 1) * P], ident_f[:]))
                 for x in range(2)
             ]
 
-        def stage_k(u, eng):
+        def stage_k(u):
             at_ps = live[("at", u)]
             ag = ap3.tile([P, P, 2], F32, name="ag", align_bytes=64)
-            copy_on(eng, ag[:], at_ps[:].rearrange("p u q -> p q u"))
+            copy_on(K_ENG, ag[:], at_ps[:].rearrange("p u q -> p q u"))
             live[("ag", u)] = ag
 
         def stage_l(u):
@@ -324,14 +387,15 @@ def tile_mmattn_pb_t_kernel(tc, q_rot, k_rot, v, w_out1, b_out1, w_out2, b_out2,
             a_codes = ap3.tile([P, P], U32, name="a_codes", align_bytes=64)
             a_scales = ap3.tile([P, P], U8, name="a_scales", align_bytes=64)
             nc.vector.quantize_mx(
-                out=a_codes[:].bitcast(FP8X4), scales=a_scales[:], in_=ag[:].rearrange("p q u -> p (q u)").bitcast(BF16)
+                out=a_codes[:].bitcast(FP8X4), scales=a_scales[:],
+                in_=ag[:].rearrange("p q u -> p (q u)").bitcast(BF16),
             )
             live[("ac", u)] = (a_codes, a_scales)
 
         def stage_m(st, u):
             s = (u % 8) // 4
             a_codes, a_scales = live[("ac", u)]
-            o_ps = misc_bank(st, [P, D], F32, "o_ps")
+            o_ps = misc_bank(st, "o", [P, D], F32, "o_ps")
             live[("o", u)] = o_ps
             return [
                 lambda: nc.tensor.matmul_mx(
@@ -350,29 +414,6 @@ def tile_mmattn_pb_t_kernel(tc, q_rot, k_rot, v, w_out1, b_out1, w_out2, b_out2,
             nc.vector.tensor_tensor(out=o_sb[:], in0=o_ps[:], in1=bias_f[:, s, :], op=ALU.add)
             nc.sync.dma_start(out=outs[s][b, (u % 4) * P:(u % 4 + 1) * P, :], in_=o_sb[:])
 
-        def weave(mms, ds, mxs, ts):
-            per = 3
-            pos = 0
-            if not mms or not TS_EARLY:
-                for mm in mms:
-                    mm()
-                    for f in ds[pos:pos + per]:
-                        f()
-                    pos += per
-                for f in ds[pos:] + mxs + ts:
-                    f()
-                return
-            for mm in mms[:3]:
-                mm()
-                for f in ds[pos:pos + per]:
-                    f()
-                pos += per
-            for f in ds[pos:] + ts:
-                f()
-            mms[3]()
-            for f in mxs:
-                f()
-
         def due(st, off):
             if st >= off and (st - off) % 2 == 0 and (st - off) // 2 < PAIRS:
                 return (st - off) // 2
@@ -380,64 +421,89 @@ def tile_mmattn_pb_t_kernel(tc, q_rot, k_rot, v, w_out1, b_out1, w_out2, b_out2,
 
         for n in range(4):
             x, h, a = GROUPS[n]
-            trs, evac = qk_group(-1, x, 0, h, a)
+            trs, evac = qk_group(-1, "qk", x, 0, h, a)
             for f in trs:
                 f()
             evac("v" if n % 2 == 0 else "s")
 
-        for st in range(UNITS + OFF_M - 1):
+        for st in range(UNITS + max(OFF_M, OFF_N) + 1):
             b16, r16 = divmod(st, 16)
-            tail = TAIL_S and st >= UNITS
-            mms, ds, mxs, ts = [], [], [], []
-            post_s, post_v = [], []
-            if st < UNITS:
-                mms = stage_a(st)
-            if r16 == 4 and b16 + 2 < B:
+            ug, ur, uh, ui = due(st, OFF_G), due(st, OFF_R), due(st, OFF_H), due(st, OFF_I)
+            uj, uk, ul, um, un = due(st, OFF_J), due(st, OFF_K), due(st, OFF_L), due(st, OFF_M), due(st, OFF_N)
+            pe = {"a0": [], "D": [], "Q": [], "J": [], "H": [], "M": []}
+            mms = stage_a(st) if st < UNITS else [None] * 4
+            for n in range(4):
+                pe["a%d" % n] = [mms[n]] if mms[n] else []
+            evacs = []
+            if 0 <= st - OFF_D < UNITS:
+                pe["D"] = stage_d(st - OFF_D)
+            for n in range(4):
+                pe["D%d" % n] = pe["D"][n:n + 1]
+            for b, gi, kind in qk_plan.get(st, []):
+                x, h, a = GROUPS[gi]
+                trs, evac = qk_group(st, kind, x, b, h, a)
+                pe["Q"] += trs
+                evacs.append(evac)
+            if uj is not None:
+                pe["J"] = stage_j(st, uj)
+            if uh is not None:
+                pe["H"] = stage_h(st, uh)
+            if um is not None:
+                pe["M"] = stage_m(st, um)
+            for key in PE_ORDER:
+                for f in pe[key]:
+                    f()
+            if st < UNITS and r16 == 7 and b16 + 2 < B:
                 load_batch(b16 + 2)
-            if st == 6:
-                post_v.append(prep_w)
-            if 0 <= st - 2 < UNITS:
-                ds += stage_d(st - 2)
-                if tail and st % 2 == 1:
-                    post_v.append(lambda: stage_e(st - 2, "v"))
-                else:
-                    post_s.append(lambda: stage_e(st - 2, "s"))
             if st < UNITS and r16 < 4:
                 v_regroup(b16, r16 // 2, r16 % 2)
-            if st < UNITS and r16 in (2, 4):
-                post_v.append(lambda: v_quant(b16, r16 // 2 - 1))
-            for n, (b, gi) in enumerate(qk_plan.get(st, [])):
-                x, h, a = GROUPS[gi]
-                trs, evac = qk_group(st, x, b, h, a)
-                ts += trs
-                if st > 0 and (QK_S_EVERY == 0 or (st // 2 + n) % QK_S_EVERY != 0):
-                    post_v.append(lambda evac=evac: evac("v"))
-                else:
-                    post_s.append(lambda evac=evac: evac("s"))
-            ug, uh, uj, ul, um = due(st, OFF_G), due(st, OFF_H), due(st, OFF_J), due(st, OFF_L), due(st, OFF_M)
-            if ug is not None:
-                post_v += stage_gq(ug)
-            if uh is not None:
-                mxs += stage_h(st, uh)
-                post_s += stage_i(uh, "s")
-            if uj is not None:
-                ts += stage_j(st, uj)
-                post_s.append(lambda: stage_k(uj, "s"))
-            if ul is not None:
-                post_v.append(lambda: stage_l(ul))
-            if um is not None:
-                mxs += stage_m(st, um)
-                post_v.append(lambda: stage_n(um))
-            weave(mms, ds, mxs, ts)
             if st < UNITS:
                 stage_b(st)
-                for f in post_v[:GAP]:
-                    f()
-                post_v = post_v[GAP:]
-                stage_b2(st)
-            for f in post_s:
-                f()
+            if ug is not None:
+                stage_sum(ug)
+            if ur is not None:
+                stage_recip(ur)
             if st < UNITS:
-                stage_c(st)
-            for f in post_v:
-                f()
+                stage_b2(st)
+            go = stage_i(ui) if ui is not None else None
+            late_v = []
+            for key in S_ORDER:
+                if key == "E" and 0 <= st - OFF_E < UNITS:
+                    stage_e(st - OFF_E, "v" if st == UNITS + 1 else E_ENG[st % 2])
+                if key == "I" and go:
+                    for h in range(2):
+                        eng = TAIL_I[h] if st >= UNITS else I_ENG[h]
+                        if eng == "s":
+                            go(h, "s")
+                        else:
+                            late_v.append(lambda h=h, go=go: go(h, "v"))
+                if key == "K" and uk is not None:
+                    stage_k(uk)
+                if key == "C" and st < UNITS:
+                    if st == 0 and EARLY_Q == 1:
+                        evacs[0]("s")
+                        evacs = evacs[1:]
+                    stage_c(st)
+                if key == "Q" and Q_ENG == "s":
+                    for evac in evacs:
+                        evac("s")
+            for key in V_ORDER:
+                if key == "L" and ul is not None:
+                    stage_l(ul)
+                if key == "N" and un is not None:
+                    stage_n(un)
+                if key == "G" and ug is not None:
+                    stage_g(ug)
+                if key == "I":
+                    for f in late_v:
+                        f()
+                if key == "Q" and Q_ENG == "v":
+                    for evac in evacs:
+                        evac("s" if st == 0 and EARLY_Q == 0 else "v")
+            if st < UNITS and r16 in (2, 4):
+                v_quant(b16, r16 // 2 - 1)
+            for s in range(2):
+                if st == PW[s]:
+                    prep_w0(s)
+                if st == PW[s] + 3:
+                    prep_w(s)

@@ -24,7 +24,7 @@ OFF_D, OFF_E = 2, 2
 QK_PAR = 3
 BANKS = {"s": ("s", 4), "et": ("et", 1), "pv": ("pv", 1), "qk": ("qk", 1), "at": ("ao", 1), "o": ("ao", 1)}
 PE_ORDER = ["a0", "a1", "D", "Q", "J", "a2", "a3", "H", "M"]
-V_ORDER = ["L", "N", "G", "Q"]
+V_ORDER = ["L", "N", "G0", "G1", "Q"]
 S_ORDER = ["E", "I", "K", "C"]
 FILL = ["sum", "recip"]
 I_ENG = ("s", "s")
@@ -40,24 +40,25 @@ EARLY_Q = 0
 LOADS = 0
 LATE_KIND = "at"
 
-BANKS = {"s": ("s", 4,), "et": ("et", 1,), "pv": ("pv", 1,), "qk": ("x", 2,), "at": ("x", 2,), "o": ("x", 2,)}
+BANKS = {"s": ("s", 4,), "et": ("et", 2,), "pv": ("p", 1,), "qk": ("q", 1,), "at": ("p", 1,), "o": ("q", 1,)}
 OFF_G = 4
 OFF_R = 5
 OFF_H = 6
 OFF_I = 6
 OFF_J = 9
 OFF_K = 9
-OFF_L = 12
-OFF_M = 16
-OFF_N = 16
+OFF_L = 11
+OFF_M = 14
+OFF_N = 14
 QK_PAR = 3
-PE_ORDER = ("a0", "a1", "a2", "a3", "D", "Q", "J", "H", "M",)
-V_ORDER = ("G", "L", "I", "Q", "N",)
-S_ORDER = ("E", "I", "K", "C",)
-EARLY_Q = 1
+PE_ORDER = ("a0", "a1", "D0", "D1", "a2", "D2", "D3", "a3", "Q", "J", "H", "M",)
+V_ORDER = ("sum", "L", "recip", "G1", "N",)
+FILL = ("Q", "G0",)
+S_ORDER = ("I", "E", "K", "C",)
+EARLY_Q = 0
 TAIL_I = ("s", "s",)
-SWAP = True
-PW = (6, 10,)
+SWAP = False
+PW = (4, 6,)
 PW_ENG = "g"
 I_ENG = ("s", "s",)
 Q_ENG = "v"
@@ -321,11 +322,10 @@ def tile_mmattn_pb_t_kernel(tc, q_rot, k_rot, v, w_out1, b_out1, w_out2, b_out2,
             e_codes = gp.tile([P, 4 * P], U32, name="e_codes", align_bytes=64)
             e_scales = gp.tile([P, 4 * P], U8, name="e_scales", align_bytes=64)
             live[("ec", u)] = (e_codes, e_scales)
-            for h in range(H):
-                nc.vector.quantize_mx(
-                    out=e_codes[:, h * 256:(h + 1) * 256].bitcast(FP8X4), scales=e_scales[:, h * 256:(h + 1) * 256],
-                    in_=live[("eg", u, h)][:].rearrange("p g q u -> p (g q u)").bitcast(BF16),
-                )
+            return lambda h: nc.vector.quantize_mx(
+                out=e_codes[:, h * 256:(h + 1) * 256].bitcast(FP8X4), scales=e_scales[:, h * 256:(h + 1) * 256],
+                in_=live[("eg", u, h)][:].rearrange("p g q u -> p (g q u)").bitcast(BF16),
+            )
 
         def stage_h(st, u):
             b = u // 8
@@ -350,11 +350,11 @@ def tile_mmattn_pb_t_kernel(tc, q_rot, k_rot, v, w_out1, b_out1, w_out2, b_out2,
 
         def stage_i(u):
             pv = live[("pv", u)]
-            rinv = live[("rinv", u)]
             attn = ap3.tile([P, H * DH], BF16, name="attn")
             live[("attn", u)] = attn
             dst = attn[:].rearrange("p (u h x) -> p u h x", u=2, h=H)
             def go(h, eng):
+                rinv = live[("rinv", u)]
                 if eng == "s":
                     nc.scalar.activation(
                         out=dst[:, :, h, :], in_=pv[:, h, :].rearrange("p (u x) -> p u x", u=2), func=ACT.Copy,
@@ -459,24 +459,40 @@ def tile_mmattn_pb_t_kernel(tc, q_rot, k_rot, v, w_out1, b_out1, w_out2, b_out2,
                 v_regroup(b16, r16 // 2, r16 % 2)
             if st < UNITS:
                 stage_b(st)
-            if ug is not None:
-                stage_sum(ug)
-            if ur is not None:
-                stage_recip(ur)
+            go = stage_i(ui) if ui is not None else None
+            i_eng = TAIL_I if st >= UNITS else I_ENG
+            gq = stage_g(ug) if ug is not None else None
+
+            def vec(key):
+                if key == "sum" and ug is not None:
+                    stage_sum(ug)
+                if key == "recip" and ur is not None:
+                    stage_recip(ur)
+                if key == "L" and ul is not None:
+                    stage_l(ul)
+                if key == "N" and un is not None:
+                    stage_n(un)
+                if key in ("G0", "G1") and gq:
+                    gq(int(key[1]))
+                if key == "I":
+                    for h in range(2):
+                        if go and i_eng[h] == "v":
+                            go(h, "v")
+                if key == "Q" and Q_ENG == "v":
+                    for evac in evacs:
+                        evac("s" if st == 0 and EARLY_Q == 0 else "v")
+
+            for key in FILL:
+                vec(key)
             if st < UNITS:
                 stage_b2(st)
-            go = stage_i(ui) if ui is not None else None
-            late_v = []
             for key in S_ORDER:
                 if key == "E" and 0 <= st - OFF_E < UNITS:
                     stage_e(st - OFF_E, "v" if st == UNITS + 1 else E_ENG[st % 2])
                 if key == "I" and go:
                     for h in range(2):
-                        eng = TAIL_I[h] if st >= UNITS else I_ENG[h]
-                        if eng == "s":
+                        if i_eng[h] == "s":
                             go(h, "s")
-                        else:
-                            late_v.append(lambda h=h, go=go: go(h, "v"))
                 if key == "K" and uk is not None:
                     stage_k(uk)
                 if key == "C" and st < UNITS:
@@ -488,18 +504,7 @@ def tile_mmattn_pb_t_kernel(tc, q_rot, k_rot, v, w_out1, b_out1, w_out2, b_out2,
                     for evac in evacs:
                         evac("s")
             for key in V_ORDER:
-                if key == "L" and ul is not None:
-                    stage_l(ul)
-                if key == "N" and un is not None:
-                    stage_n(un)
-                if key == "G" and ug is not None:
-                    stage_g(ug)
-                if key == "I":
-                    for f in late_v:
-                        f()
-                if key == "Q" and Q_ENG == "v":
-                    for evac in evacs:
-                        evac("s" if st == 0 and EARLY_Q == 0 else "v")
+                vec(key)
             if st < UNITS and r16 in (2, 4):
                 v_quant(b16, r16 // 2 - 1)
             for s in range(2):

@@ -38,6 +38,10 @@ TAIL_I = ("s", "v")
 TAIL_K = "s"
 EARLY_Q = 0
 LOADS = 0
+VQ0, VQB = 2, 8
+VG_BUFS = 1
+NEG_ENG = "v"
+SUM_ENG = "v"
 LATE_KIND = "at"
 
 BANKS = {"s": ("s", 4,), "et": ("et", 2,), "pv": ("p", 1,), "qk": ("q", 1,), "at": ("p", 1,), "o": ("q", 1,)}
@@ -72,6 +76,7 @@ def tile_mmattn_pb_t_kernel(tc, q_rot, k_rot, v, w_out1, b_out1, w_out2, b_out2,
         consts = ctx.enter_context(tc.tile_pool(name="consts", bufs=1))
         raw = ctx.enter_context(tc.tile_pool(name="raw", bufs=2))
         xt = ctx.enter_context(tc.tile_pool(name="xt", bufs=2))
+        vg = ctx.enter_context(tc.tile_pool(name="vg", bufs=VG_BUFS))
         vq = ctx.enter_context(tc.tile_pool(name="vq", bufs=2))
         ep = ctx.enter_context(tc.tile_pool(name="ep", bufs=4))
         gp = ctx.enter_context(tc.tile_pool(name="gp", bufs=3))
@@ -208,25 +213,33 @@ def tile_mmattn_pb_t_kernel(tc, q_rot, k_rot, v, w_out1, b_out1, w_out2, b_out2,
         vcs = {}
 
         def v_regroup(b, h, g):
-            if g == 0:
-                v_grp = vq.tile([P, 2, DH, 4], BF16, name="v_grp%d" % h, align_bytes=64)
-                vcs[("g", b, h)] = v_grp
-            v_grp = vcs[("g", b, h)]
-            dst = v_grp[:, g].rearrange("p (u x e) j -> p u x e j", u=2, e=2)
+            v_grp = vg.tile([P, DH, 4], BF16, name="v_grp", align_bytes=64)
+            vcs[("g", b, h, g)] = v_grp
+            dst = v_grp[:].rearrange("p (u x e) j -> p u x e j", u=2, e=2)
             src = raws[("v", b, h)][:, g].rearrange("p j (x u e) -> p u x e j", u=2, e=2)
             for u in range(2):
                 nc.gpsimd.tensor_scalar(
                     out=dst[:, u], in0=src[:, u], scalar1=1.0, scalar2=0.0, op0=ALU.mult, op1=ALU.add,
                 )
 
-        def v_quant(b, h):
-            v_codes = vq.tile([P, 2 * DH], U32, name="v_codes%d" % h, align_bytes=64)
-            v_scales = vq.tile([P, 2 * DH], U8, name="v_scales%d" % h, align_bytes=64)
+        def v_quant(b, h, g):
+            if g == 0:
+                v_codes = vq.tile([P, 2 * DH], U32, name="v_codes%d" % h, align_bytes=64)
+                v_scales = vq.tile([P, 2 * DH], U8, name="v_scales%d" % h, align_bytes=64)
+                vcs[("c", b, h)] = (v_codes, v_scales)
+            v_codes, v_scales = vcs[("c", b, h)]
             nc.vector.quantize_mx(
-                out=v_codes[:].bitcast(FP8X4), scales=v_scales[:],
-                in_=vcs[("g", b, h)][:].rearrange("p g d j -> p (g d j)"),
+                out=v_codes[:, g * DH:(g + 1) * DH].bitcast(FP8X4), scales=v_scales[:, g * DH:(g + 1) * DH],
+                in_=vcs[("g", b, h, g)][:].rearrange("p d j -> p (d j)"),
             )
-            vcs[("c", b, h)] = (v_codes, v_scales)
+
+        V_PLAN = {}
+        for n in range(4):
+            V_PLAN[n + VQ0] = [(0, n // 2, n % 2)]
+            for b in range(1, B):
+                V_PLAN[16 * (b - 1) + VQB + 2 * n] = [(b, n // 2, n % 2)]
+        V_SEQ = [c for st in sorted(V_PLAN) for c in V_PLAN[st]]
+        v_next = {V_SEQ[n]: V_SEQ[n + 1] for n in range(len(V_SEQ) - 1)}
 
         live = {}
 
@@ -271,7 +284,7 @@ def tile_mmattn_pb_t_kernel(tc, q_rot, k_rot, v, w_out1, b_out1, w_out2, b_out2,
         def stage_b2(i):
             m2 = live[("m2", i)]
             negmax = st4.tile([P, 1], F32, name="negmax")
-            nc.vector.tensor_scalar(
+            (nc.vector if NEG_ENG == "v" else nc.gpsimd).tensor_scalar(
                 out=negmax[:], in0=m2[:, 0:1], scalar1=m2[:, 1:2], scalar2=-SCALE, op0=ALU.max, op1=ALU.mult
             )
             live[("negmax", i)] = negmax
@@ -311,7 +324,11 @@ def tile_mmattn_pb_t_kernel(tc, q_rot, k_rot, v, w_out1, b_out1, w_out2, b_out2,
             rs = live[("rs", u)]
             rsum = st4.tile([P, 2], F32, name="rsum")
             live[("rsum", u)] = rsum
-            nc.vector.tensor_reduce(out=rsum[:], in_=rs[:].rearrange("p (h g) -> p h g", g=2), axis=AX.X, op=ALU.add)
+            if SUM_ENG == "v":
+                nc.vector.tensor_reduce(out=rsum[:], in_=rs[:].rearrange("p (h g) -> p h g", g=2), axis=AX.X, op=ALU.add)
+            else:
+                two = rs[:].rearrange("p (h g) -> p h g", g=2)
+                nc.gpsimd.tensor_tensor(out=rsum[:], in0=two[:, :, 0], in1=two[:, :, 1], op=ALU.add)
 
         def stage_recip(u):
             rinv = st4.tile([P, 2], F32, name="rinv")
@@ -426,6 +443,8 @@ def tile_mmattn_pb_t_kernel(tc, q_rot, k_rot, v, w_out1, b_out1, w_out2, b_out2,
                 f()
             evac("v" if n % 2 == 0 else "s")
 
+        v_regroup(*V_SEQ[0])
+
         for st in range(UNITS + max(OFF_M, OFF_N) + 1):
             b16, r16 = divmod(st, 16)
             ug, ur, uh, ui = due(st, OFF_G), due(st, OFF_R), due(st, OFF_H), due(st, OFF_I)
@@ -455,8 +474,6 @@ def tile_mmattn_pb_t_kernel(tc, q_rot, k_rot, v, w_out1, b_out1, w_out2, b_out2,
                     f()
             if st < UNITS and r16 == 7 and b16 + 2 < B:
                 load_batch(b16 + 2)
-            if st < UNITS and r16 < 4:
-                v_regroup(b16, r16 // 2, r16 % 2)
             if st < UNITS:
                 stage_b(st)
             go = stage_i(ui) if ui is not None else None
@@ -468,6 +485,8 @@ def tile_mmattn_pb_t_kernel(tc, q_rot, k_rot, v, w_out1, b_out1, w_out2, b_out2,
                     stage_sum(ug)
                 if key == "recip" and ur is not None:
                     stage_recip(ur)
+                if key == "K" and uk is not None and K_ENG == "v":
+                    stage_k(uk)
                 if key == "L" and ul is not None:
                     stage_l(ul)
                 if key == "N" and un is not None:
@@ -493,7 +512,7 @@ def tile_mmattn_pb_t_kernel(tc, q_rot, k_rot, v, w_out1, b_out1, w_out2, b_out2,
                     for h in range(2):
                         if i_eng[h] == "s":
                             go(h, "s")
-                if key == "K" and uk is not None:
+                if key == "K" and uk is not None and K_ENG == "s":
                     stage_k(uk)
                 if key == "C" and st < UNITS:
                     if st == 0 and EARLY_Q == 1:
@@ -505,8 +524,10 @@ def tile_mmattn_pb_t_kernel(tc, q_rot, k_rot, v, w_out1, b_out1, w_out2, b_out2,
                         evac("s")
             for key in V_ORDER:
                 vec(key)
-            if st < UNITS and r16 in (2, 4):
-                v_quant(b16, r16 // 2 - 1)
+            for c in V_PLAN.get(st, []):
+                v_quant(*c)
+                if c in v_next:
+                    v_regroup(*v_next[c])
             for s in range(2):
                 if st == PW[s]:
                     prep_w0(s)

@@ -38,15 +38,20 @@ TAIL_I = ("s", "v")
 TAIL_K = "s"
 EARLY_Q = 0
 LOADS = 0
+WARM = (0, 0)
 VQ0, VQB = 2, 8
 VG_BUFS = 1
 NEG_ENG = "v"
 SUM_ENG = "v"
+SUM2 = False
+OFF_SUM = 4
+K_V = 1000
+I_V = 1000
 LATE_KIND = "at"
 
 BANKS = {"s": ("s", 4,), "et": ("et", 2,), "pv": ("p", 1,), "qk": ("q", 1,), "at": ("p", 1,), "o": ("q", 1,)}
 OFF_G = 4
-OFF_R = 5
+OFF_R = 4
 OFF_H = 6
 OFF_I = 6
 OFF_J = 9
@@ -55,10 +60,10 @@ OFF_L = 11
 OFF_M = 14
 OFF_N = 14
 QK_PAR = 3
-PE_ORDER = ("a0", "a1", "D0", "D1", "a2", "D2", "D3", "a3", "Q", "J", "H", "M",)
-V_ORDER = ("sum", "L", "recip", "G1", "N",)
-FILL = ("Q", "G0",)
-S_ORDER = ("I", "E", "K", "C",)
+PE_ORDER = ("a0", "D0", "a1", "D1", "a2", "D2", "a3", "D3", "H", "M", "Q", "J",)
+V_ORDER = ("G1", "recip", "N", "L", "K", "I",)
+FILL = ("Q", "sum", "G0",)
+S_ORDER = ("E", "I", "K", "C",)
 EARLY_Q = 0
 TAIL_I = ("s", "s",)
 SWAP = False
@@ -66,6 +71,10 @@ PW = (4, 6,)
 PW_ENG = "g"
 I_ENG = ("s", "s",)
 Q_ENG = "v"
+K_V = 2
+VG_BUFS = 2
+LOADS = 1
+WARM = (4, 2,)
 
 
 def tile_mmattn_pb_t_kernel(tc, q_rot, k_rot, v, w_out1, b_out1, w_out2, b_out2, out_0, out_1):
@@ -93,7 +102,7 @@ def tile_mmattn_pb_t_kernel(tc, q_rot, k_rot, v, w_out1, b_out1, w_out2, b_out2,
 
         raws = {}
 
-        def load(x, b, h, halves):
+        def load(x, b, h, halves, cs=None):
             if (x, b, h) not in raws:
                 t = raw.tile([P, 2, 4, DH], BF16, name="raw_%s%d" % (x, h))
                 raws[(x, b, h)] = t
@@ -102,7 +111,9 @@ def tile_mmattn_pb_t_kernel(tc, q_rot, k_rot, v, w_out1, b_out1, w_out2, b_out2,
                 view = srcs[x][b, h].rearrange("(a c p) d -> p a c d", a=2, c=4)
             else:
                 view = srcs[x][b, h].rearrange("(a p c) d -> p a c d", a=2, c=4)
-            if len(halves) == 2:
+            if cs is not None:
+                nc.sync.dma_start(out=t[:, 0, cs[0]:cs[1]], in_=view[:, 0, cs[0]:cs[1]])
+            elif len(halves) == 2:
                 nc.sync.dma_start(out=t[:], in_=view)
             else:
                 a = halves[0]
@@ -121,12 +132,15 @@ def tile_mmattn_pb_t_kernel(tc, q_rot, k_rot, v, w_out1, b_out1, w_out2, b_out2,
                 load("k", 0, h, (0,))
                 load("k", 0, h, (1,))
         else:
-            load("k", 0, 0, (0,))
-            load("q", 0, 0, (0,))
-            load("k", 0, 0, (1,))
-            load("k", 0, 1, (0,))
-            load("k", 0, 1, (1,))
+            load("q", 0, 0, (0,), (0, 1))
+            for h in range(H):
+                for a in range(2):
+                    load("k", 0, h, (a,))
+                if LOADS == 2 and h == 0:
+                    load("q", 0, 0, (0,), (1, 4))
             load("q", 0, 1, (0,))
+            if LOADS == 1:
+                load("q", 0, 0, (0,), (1, 4))
         for h in range(H):
             load("v", 0, h, (0, 1))
         load("q", 1, 0, (0, 1))
@@ -180,22 +194,23 @@ def tile_mmattn_pb_t_kernel(tc, q_rot, k_rot, v, w_out1, b_out1, w_out2, b_out2,
 
         xts = {}
 
-        def qk_group(st, kind, x, b, h, a):
+        def qk_group(st, kind, x, b, h, a, cs=(0, 1, 2, 3)):
             src = raws[(x, b, h)]
             if (x, b, h) not in xts:
                 t = xt.tile([P, 8 * P], F32, name="xt_%s%d" % (x, h))
                 xts[(x, b, h)] = t
             dst = xts[(x, b, h)]
-            bank = misc_bank(st, kind, [P, 4, P], F32, "bank_x")
+            nt = len(cs)
+            bank = misc_bank(st, kind, [P, nt, P], F32, "bank_x")
             trs = [
-                (lambda c=c: nc.tensor.transpose(bank[:, c, :], src[:, a, c, :].bitcast(F32), ident_f[:]))
-                for c in range(4)
+                (lambda n=n, c=c: nc.tensor.transpose(bank[:, n, :], src[:, a, c, :].bitcast(F32), ident_f[:]))
+                for n, c in enumerate(cs)
             ]
-            out = dst[:, a * 512:(a + 1) * 512]
+            out = dst[:, a * 512 + cs[0] * P:a * 512 + (cs[-1] + 1) * P]
             if x == "q":
                 return trs, lambda eng: copy_on(eng, out, bank[:].rearrange("p c t -> p (c t)"))
             return trs, lambda eng: copy_on(
-                eng, out.rearrange("p (u t e) -> p u t e", u=2, e=2), bank[:].rearrange("p (u e) t -> p u t e", e=2)
+                eng, out.rearrange("p (u t e) -> p u t e", u=nt // 2, e=2), bank[:].rearrange("p (u e) t -> p u t e", e=2)
             )
 
         GROUPS = [("q", 0, 0), ("k", 0, 0), ("k", 0, 1), ("q", 1, 0), ("k", 1, 0), ("k", 1, 1), ("q", 0, 1), ("q", 1, 1)]
@@ -293,13 +308,19 @@ def tile_mmattn_pb_t_kernel(tc, q_rot, k_rot, v, w_out1, b_out1, w_out2, b_out2,
             banks = live[("s", i)]
             negmax = live[("negmax", i)]
             u, h = pair_of(i)
-            if h == 0:
-                rs = st4.tile([P, 4], F32, name="rs")
-                live[("rs", u)] = rs
-            rs = live[("rs", u)]
+            if SUM2:
+                if ("rs", u // 2) not in live:
+                    rs = st4.tile([P, 8], F32, name="rs")
+                    live[("rs", u // 2)] = rs
+                rs = live[("rs", u // 2)]
+            else:
+                if h == 0:
+                    rs = st4.tile([P, 4], F32, name="rs")
+                    live[("rs", u)] = rs
+                rs = live[("rs", u)]
             e_sb = ep.tile([P, 2, 512], BF16, name="e_sb")
             for g in range(2):
-                col = h * 2 + g
+                col = h * 2 + g + (4 * (u % 2) if SUM2 else 0)
                 nc.scalar.activation(
                     out=e_sb[:, g, :], in_=banks[g][:], func=ACT.Exp,
                     bias=negmax[:, 0:1], scale=SCALE, accum_out=rs[:, col:col + 1],
@@ -321,6 +342,14 @@ def tile_mmattn_pb_t_kernel(tc, q_rot, k_rot, v, w_out1, b_out1, w_out2, b_out2,
             live[("eg",) + pair_of(i)] = eg
 
         def stage_sum(u):
+            if SUM2:
+                if u % 2 == 0:
+                    return
+                rs = live[("rs", u // 2)]
+                rsum = st4.tile([P, 4], F32, name="rsum")
+                live[("rsum", u // 2)] = rsum
+                nc.vector.tensor_reduce(out=rsum[:], in_=rs[:].rearrange("p (h g) -> p h g", g=2), axis=AX.X, op=ALU.add)
+                return
             rs = live[("rs", u)]
             rsum = st4.tile([P, 2], F32, name="rsum")
             live[("rsum", u)] = rsum
@@ -331,6 +360,14 @@ def tile_mmattn_pb_t_kernel(tc, q_rot, k_rot, v, w_out1, b_out1, w_out2, b_out2,
                 nc.gpsimd.tensor_tensor(out=rsum[:], in0=two[:, :, 0], in1=two[:, :, 1], op=ALU.add)
 
         def stage_recip(u):
+            if SUM2:
+                if u % 2 == 0:
+                    return
+                rinv = st4.tile([P, 4], F32, name="rinv")
+                live[("rinv", u - 1)] = rinv[:, 0:2]
+                live[("rinv", u)] = rinv[:, 2:4]
+                nc.vector.reciprocal(out=rinv[:], in_=live[("rsum", u // 2)][:])
+                return
             rinv = st4.tile([P, 2], F32, name="rinv")
             live[("rinv", u)] = rinv
             nc.vector.reciprocal(out=rinv[:], in_=live[("rsum", u)][:])
@@ -394,9 +431,10 @@ def tile_mmattn_pb_t_kernel(tc, q_rot, k_rot, v, w_out1, b_out1, w_out2, b_out2,
             ]
 
         def stage_k(u):
+            eng = "v" if K_ENG == "v" or u % K_V == K_V - 1 else "s"
             at_ps = live[("at", u)]
             ag = ap3.tile([P, P, 2], F32, name="ag", align_bytes=64)
-            copy_on(K_ENG, ag[:], at_ps[:].rearrange("p u q -> p q u"))
+            copy_on(eng, ag[:], at_ps[:].rearrange("p u q -> p q u"))
             live[("ag", u)] = ag
 
         def stage_l(u):
@@ -436,18 +474,38 @@ def tile_mmattn_pb_t_kernel(tc, q_rot, k_rot, v, w_out1, b_out1, w_out2, b_out2,
                 return (st - off) // 2
             return None
 
-        for n in range(4):
-            x, h, a = GROUPS[n]
-            trs, evac = qk_group(-1, "qk", x, 0, h, a)
-            for f in trs:
-                f()
-            evac("v" if n % 2 == 0 else "s")
+        if LOADS == 0:
+            for n in range(4):
+                x, h, a = GROUPS[n]
+                trs, evac = qk_group(-1, "qk", x, 0, h, a)
+                for f in trs:
+                    f()
+                evac("v" if n % 2 == 0 else "s")
+        else:
+            if WARM[0]:
+                zeros = consts.tile([P, 512], BF16)
+                nc.vector.memset(zeros[:], 0.0)
+
+            def warm(n):
+                for k in range(n):
+                    scratch = ps["et"].tile([P, 512], F32, name="scratch", tag="et")
+                    nc.tensor.matmul(out=scratch[:], lhsT=zeros[:, 0:P], rhs=zeros[:], start=True, stop=True)
+
+            warm(WARM[0])
+            for k, (x, a, cs, eng) in enumerate((("q", 0, (0,), "v"), ("k", 0, (0, 1), "v"), ("k", 0, (2, 3), "s"), ("k", 1, (0, 1), "v"), ("k", 1, (2, 3), "s"))):
+                if k == 3:
+                    warm(WARM[1])
+                trs, evac = qk_group(-1, "qk", x, 0, 0, a, cs)
+                for f in trs:
+                    f()
+                evac(eng)
 
         v_regroup(*V_SEQ[0])
 
         for st in range(UNITS + max(OFF_M, OFF_N) + 1):
             b16, r16 = divmod(st, 16)
             ug, ur, uh, ui = due(st, OFF_G), due(st, OFF_R), due(st, OFF_H), due(st, OFF_I)
+            usum = due(st, OFF_SUM)
             uj, uk, ul, um, un = due(st, OFF_J), due(st, OFF_K), due(st, OFF_L), due(st, OFF_M), due(st, OFF_N)
             pe = {"a0": [], "D": [], "Q": [], "J": [], "H": [], "M": []}
             mms = stage_a(st) if st < UNITS else [None] * 4
@@ -458,9 +516,13 @@ def tile_mmattn_pb_t_kernel(tc, q_rot, k_rot, v, w_out1, b_out1, w_out2, b_out2,
                 pe["D"] = stage_d(st - OFF_D)
             for n in range(4):
                 pe["D%d" % n] = pe["D"][n:n + 1]
-            for b, gi, kind in qk_plan.get(st, []):
-                x, h, a = GROUPS[gi]
-                trs, evac = qk_group(st, kind, x, b, h, a)
+            todo = [(b, kind) + GROUPS[gi] for b, gi, kind in qk_plan.get(st, [])]
+            if st == 0 and LOADS == 2:
+                todo = [(0, "qk", "q", 0, 0, (1, 2, 3)), (0, "pv", "k", 1, 0), (0, "et", "k", 1, 1), (0, "et", "q", 1, 0)]
+            elif st == 0 and LOADS:
+                todo = [(0, "qk", "k", 1, 0), (0, "pv", "k", 1, 1), (0, "et", "q", 1, 0), (0, "et", "q", 0, 0, (1, 2, 3))]
+            for b, kind, x, h, a, *cs in todo:
+                trs, evac = qk_group(st, kind, x, b, h, a, *cs)
                 pe["Q"] += trs
                 evacs.append(evac)
             if uj is not None:
@@ -469,6 +531,10 @@ def tile_mmattn_pb_t_kernel(tc, q_rot, k_rot, v, w_out1, b_out1, w_out2, b_out2,
                 pe["H"] = stage_h(st, uh)
             if um is not None:
                 pe["M"] = stage_m(st, um)
+            for nm in ("Q", "J", "H"):
+                for n in range(4):
+                    pe["%s%d" % (nm, n)] = pe[nm][n:n + 1]
+            pe["Q4"] = pe["Q"][4:]
             for key in PE_ORDER:
                 for f in pe[key]:
                     f()
@@ -477,15 +543,15 @@ def tile_mmattn_pb_t_kernel(tc, q_rot, k_rot, v, w_out1, b_out1, w_out2, b_out2,
             if st < UNITS:
                 stage_b(st)
             go = stage_i(ui) if ui is not None else None
-            i_eng = TAIL_I if st >= UNITS else I_ENG
+            i_eng = TAIL_I if st >= UNITS else ("s", "v") if ui is not None and ui % I_V == I_V - 1 else I_ENG
             gq = stage_g(ug) if ug is not None else None
 
             def vec(key):
-                if key == "sum" and ug is not None:
-                    stage_sum(ug)
+                if key == "sum" and usum is not None:
+                    stage_sum(usum)
                 if key == "recip" and ur is not None:
                     stage_recip(ur)
-                if key == "K" and uk is not None and K_ENG == "v":
+                if key == "K" and uk is not None and (K_ENG == "v" or uk % K_V == K_V - 1):
                     stage_k(uk)
                 if key == "L" and ul is not None:
                     stage_l(ul)
@@ -502,7 +568,8 @@ def tile_mmattn_pb_t_kernel(tc, q_rot, k_rot, v, w_out1, b_out1, w_out2, b_out2,
                         evac("s" if st == 0 and EARLY_Q == 0 else "v")
 
             for key in FILL:
-                vec(key)
+                if not (st == 0 and LOADS):
+                    vec(key)
             if st < UNITS:
                 stage_b2(st)
             for key in S_ORDER:
@@ -512,18 +579,34 @@ def tile_mmattn_pb_t_kernel(tc, q_rot, k_rot, v, w_out1, b_out1, w_out2, b_out2,
                     for h in range(2):
                         if i_eng[h] == "s":
                             go(h, "s")
-                if key == "K" and uk is not None and K_ENG == "s":
+                if key == "K" and uk is not None and K_ENG == "s" and uk % K_V != K_V - 1:
                     stage_k(uk)
                 if key == "C" and st < UNITS:
-                    if st == 0 and EARLY_Q == 1:
+                    if st == 0 and LOADS == 2:
+                        pass
+                    elif st == 0 and LOADS:
+                        evacs[0]("s")
+                        evacs[1]("s")
+                    elif st == 0 and EARLY_Q == 1:
                         evacs[0]("s")
                         evacs = evacs[1:]
                     stage_c(st)
                 if key == "Q" and Q_ENG == "s":
                     for evac in evacs:
                         evac("s")
+            if st == 0 and LOADS == 2:
+                evacs[0]("v")
+                evacs[1]("s")
+                evacs[2]("s")
+                late_q = evacs[3]
+            elif st == 1 and LOADS == 2:
+                late_q("v")
+            elif st == 0 and LOADS:
+                evacs[2]("v")
+                evacs[3]("v")
             for key in V_ORDER:
-                vec(key)
+                if not (st == 0 and LOADS):
+                    vec(key)
             for c in V_PLAN.get(st, []):
                 v_quant(*c)
                 if c in v_next:

@@ -39,7 +39,7 @@ TAIL_K = "s"
 EARLY_Q = 0
 LOADS = 0
 WARM = (0, 0)
-VQ0, VQB = 2, 8
+VQ0, VQB, VQS = 2, 6, 1
 VG_BUFS = 1
 NEG_ENG = "v"
 SUM_ENG = "v"
@@ -60,7 +60,7 @@ OFF_L = 11
 OFF_M = 14
 OFF_N = 14
 QK_PAR = 3
-PE_ORDER = ("a0", "D0", "a1", "D1", "a2", "D2", "a3", "D3", "H", "M", "Q", "J",)
+PE_ORDER = ("a0", "D0", "a1", "D1", "a2", "D2", "D3", "a3", "H", "M", "Q", "J",)
 V_ORDER = ("G1", "recip", "N", "L", "K", "I",)
 FILL = ("Q", "sum", "G0",)
 S_ORDER = ("E", "I", "K", "C",)
@@ -74,7 +74,7 @@ Q_ENG = "v"
 K_V = 2
 VG_BUFS = 2
 LOADS = 1
-WARM = (4, 2,)
+WARM = (3, 2,)
 
 
 def tile_mmattn_pb_t_kernel(tc, q_rot, k_rot, v, w_out1, b_out1, w_out2, b_out2, out_0, out_1):
@@ -227,34 +227,35 @@ def tile_mmattn_pb_t_kernel(tc, q_rot, k_rot, v, w_out1, b_out1, w_out2, b_out2,
 
         vcs = {}
 
-        def v_regroup(b, h, g):
-            v_grp = vg.tile([P, DH, 4], BF16, name="v_grp", align_bytes=64)
-            vcs[("g", b, h, g)] = v_grp
-            dst = v_grp[:].rearrange("p (u x e) j -> p u x e j", u=2, e=2)
-            src = raws[("v", b, h)][:, g].rearrange("p j (x u e) -> p u x e j", u=2, e=2)
-            for u in range(2):
-                nc.gpsimd.tensor_scalar(
-                    out=dst[:, u], in0=src[:, u], scalar1=1.0, scalar2=0.0, op0=ALU.mult, op1=ALU.add,
-                )
+        def v_regroup(b, h, g, u):
+            v_grp = vg.tile([P, DH // 2, 4], BF16, name="v_grp", align_bytes=64)
+            vcs[("g", b, h, g, u)] = v_grp
+            nc.gpsimd.tensor_scalar(
+                out=v_grp[:].rearrange("p (x e) j -> p x e j", e=2),
+                in0=raws[("v", b, h)][:, g].rearrange("p j (x u e) -> p u x e j", u=2, e=2)[:, u],
+                scalar1=1.0, scalar2=0.0, op0=ALU.mult, op1=ALU.add,
+            )
 
-        def v_quant(b, h, g):
-            if g == 0:
+        def v_quant(b, h, g, u):
+            if (g, u) == (0, 0):
                 v_codes = vq.tile([P, 2 * DH], U32, name="v_codes%d" % h, align_bytes=64)
                 v_scales = vq.tile([P, 2 * DH], U8, name="v_scales%d" % h, align_bytes=64)
                 vcs[("c", b, h)] = (v_codes, v_scales)
             v_codes, v_scales = vcs[("c", b, h)]
+            cols = slice((2 * g + u) * P, (2 * g + u + 1) * P)
             nc.vector.quantize_mx(
-                out=v_codes[:, g * DH:(g + 1) * DH].bitcast(FP8X4), scales=v_scales[:, g * DH:(g + 1) * DH],
-                in_=vcs[("g", b, h, g)][:].rearrange("p d j -> p (d j)"),
+                out=v_codes[:, cols].bitcast(FP8X4), scales=v_scales[:, cols],
+                in_=vcs[("g", b, h, g, u)][:].rearrange("p d j -> p (d j)"),
             )
 
         V_PLAN = {}
-        for n in range(4):
-            V_PLAN[n + VQ0] = [(0, n // 2, n % 2)]
+        for n in range(8):
+            c = (n // 4, n // 2 % 2, n % 2)
+            V_PLAN.setdefault(VQ0 + n // 2, []).append((0,) + c)
             for b in range(1, B):
-                V_PLAN[16 * (b - 1) + VQB + 2 * n] = [(b, n // 2, n % 2)]
+                V_PLAN.setdefault(16 * (b - 1) + VQB + VQS * n, []).append((b,) + c)
         V_SEQ = [c for st in sorted(V_PLAN) for c in V_PLAN[st]]
-        v_next = {V_SEQ[n]: V_SEQ[n + 1] for n in range(len(V_SEQ) - 1)}
+        v_next = {V_SEQ[n]: V_SEQ[n + VG_BUFS] for n in range(len(V_SEQ) - VG_BUFS)}
 
         live = {}
 
@@ -500,7 +501,8 @@ def tile_mmattn_pb_t_kernel(tc, q_rot, k_rot, v, w_out1, b_out1, w_out2, b_out2,
                     f()
                 evac(eng)
 
-        v_regroup(*V_SEQ[0])
+        for n in range(VG_BUFS):
+            v_regroup(*V_SEQ[n])
 
         for st in range(UNITS + max(OFF_M, OFF_N) + 1):
             b16, r16 = divmod(st, 16)

from contextlib import ExitStack

import concourse.mybir as mybir
from concourse.masks import make_identity

F32 = mybir.dt.float32
BF16 = mybir.dt.bfloat16
U32 = mybir.dt.uint32
U8 = mybir.dt.uint8
FP8X4 = mybir.dt.float8_e4m3fn_x4
ACT = mybir.ActivationFunctionType
ALU = mybir.AluOpType
AX = mybir.AxisListType

B, H, N, DH, D = 4, 2, 1024, 256, 256
P = 128
SCALE = 1.0 / 16.0
FLOPS = 2 * B * H * N * N * DH * 2 + 2 * B * N * H * DH * D

UNITS = B * 8 * H
PAIRS = UNITS // 2
OFF_G, OFF_R, OFF_H, OFF_I, OFF_J, OFF_K, OFF_L, OFF_M, OFF_N = 4, 5, 6, 7, 10, 10, 10, 11, 11
OFF_D, OFF_E = 2, 2
QK_PAR = 3
BANKS = {"s": ("s", 4), "et": ("et", 1), "pv": ("pv", 1), "qk": ("qk", 1), "at": ("ao", 1), "o": ("ao", 1)}
PE_ORDER = ["a0", "a1", "D", "Q", "J", "a2", "a3", "H", "M"]
V_ORDER = ["L", "N", "G0", "G1", "Q"]
S_ORDER = ["E", "I", "K", "C"]
FILL = ["sum", "recip"]
I_ENG = ("s", "s")
K_ENG = "s"
Q_ENG = "v"
E_ENG = ("s", "s")
SWAP = True
PW = (6, 6)
PW_ENG = "g"
TAIL_I = ("s", "v")
TAIL_K = "s"
EARLY_Q = 0
LOADS = 0
WARM = (0, 0)
VQ0, VQB, VQS = 2, 6, 1
VG_BUFS = 1
NEG_ENG = "v"
SUM_ENG = "v"
SUM2 = False
OFF_SUM = 4
K_V = 1000
I_V = 1000
LATE_KIND = "at"

BANKS = {"s": ("s", 4,), "et": ("et", 2,), "pv": ("p", 1,), "qk": ("q", 1,), "at": ("p", 1,), "o": ("q", 1,)}
OFF_G = 4
OFF_R = 4
OFF_H = 6
OFF_I = 6
OFF_J = 9
OFF_K = 9
OFF_L = 11
OFF_M = 14
OFF_N = 14
QK_PAR = 3
PE_ORDER = ("a0", "D0", "a1", "D1", "a2", "D2", "D3", "a3", "H", "M", "Q", "J",)
V_ORDER = ("G1", "recip", "N", "L", "K", "I",)
FILL = ("Q", "sum", "G0",)
S_ORDER = ("E", "I", "K", "C",)
EARLY_Q = 0
TAIL_I = ("s", "s",)
SWAP = False
PW = (4, 6,)
PW_ENG = "g"
I_ENG = ("s", "s",)
Q_ENG = "v"
K_V = 2
VG_BUFS = 2
LOADS = 1
WARM = (3, 2,)


def tile_mmattn_pb_t_kernel(tc, q_rot, k_rot, v, w_out1, b_out1, w_out2, b_out2, out_0, out_1):
    nc = tc.nc
    outs = [out_0, out_1]
    srcs = {"q": q_rot, "k": k_rot, "v": v}
    with ExitStack() as ctx:
        consts = ctx.enter_context(tc.tile_pool(name="consts", bufs=1))
        raw = ctx.enter_context(tc.tile_pool(name="raw", bufs=2))
        xt = ctx.enter_context(tc.tile_pool(name="xt", bufs=2))
        vg = ctx.enter_context(tc.tile_pool(name="vg", bufs=VG_BUFS))
        vq = ctx.enter_context(tc.tile_pool(name="vq", bufs=2))
        ep = ctx.enter_context(tc.tile_pool(name="ep", bufs=4))
        gp = ctx.enter_context(tc.tile_pool(name="gp", bufs=3))
        st4 = ctx.enter_context(tc.tile_pool(name="st4", bufs=6))
        ap3 = ctx.enter_context(tc.tile_pool(name="ap3", bufs=3))
        ps = {}
        for kind, (nm, nb) in BANKS.items():
            if nm not in ps:
                ps[nm] = ctx.enter_context(tc.psum_pool(name="ps_" + nm, bufs=nb))
        ctx.enter_context(tc.manual_schedule())

        ident_f = consts.tile([P, P], F32)
        make_identity(nc, ident_f[:])

        raws = {}

        def load(x, b, h, halves, cs=None):
            if (x, b, h) not in raws:
                t = raw.tile([P, 2, 4, DH], BF16, name="raw_%s%d" % (x, h))
                raws[(x, b, h)] = t
            t = raws[(x, b, h)]
            if x == "q":
                view = srcs[x][b, h].rearrange("(a c p) d -> p a c d", a=2, c=4)
            else:
                view = srcs[x][b, h].rearrange("(a p c) d -> p a c d", a=2, c=4)
            if cs is not None:
                nc.sync.dma_start(out=t[:, 0, cs[0]:cs[1]], in_=view[:, 0, cs[0]:cs[1]])
            elif len(halves) == 2:
                nc.sync.dma_start(out=t[:], in_=view)
            else:
                a = halves[0]
                nc.sync.dma_start(out=t[:, a], in_=view[:, a])

        def load_batch(b):
            for h in range(H):
                load("q", b, h, (0, 1))
                load("k", b, h, (0, 1))
            for h in range(H):
                load("v", b, h, (0, 1))

        if LOADS == 0:
            for h in range(H):
                load("q", 0, h, (0,))
                load("k", 0, h, (0,))
                load("k", 0, h, (1,))
        else:
            load("q", 0, 0, (0,), (0, 1))
            for h in range(H):
                for a in range(2):
                    load("k", 0, h, (a,))
                if LOADS == 2 and h == 0:
                    load("q", 0, 0, (0,), (1, 4))
            load("q", 0, 1, (0,))
            if LOADS == 1:
                load("q", 0, 0, (0,), (1, 4))
        for h in range(H):
            load("v", 0, h, (0, 1))
        load("q", 1, 0, (0, 1))
        for h in range(H):
            load("q", 0, h, (1,))
        load("k", 1, 0, (0, 1))
        w_raw = consts.tile([P, 2, 4, D], BF16)
        bias_bf = consts.tile([P, 2, D], BF16)
        for s, (w, bb) in enumerate(((w_out1, b_out1), (w_out2, b_out2))):
            nc.sync.dma_start(out=w_raw[:, s], in_=w.rearrange("(p j) o -> p j o", j=4))
            nc.sync.dma_start(out=bias_bf[:, s, :], in_=bb.partition_broadcast(P))
        load("q", 1, 1, (0, 1))
        load("k", 1, 1, (0, 1))
        for h in range(H):
            load("v", 1, h, (0, 1))

        w_grp = consts.tile([P, 2, D, 4], BF16, align_bytes=64)
        w_codes = consts.tile([P, 2, D], U32, align_bytes=64)
        w_scales = consts.tile([P, 2, D], U8, align_bytes=64)
        bias_f = consts.tile([P, 2, D], F32)

        def prep_w0(s):
            src = w_raw[:, s].rearrange("p j o -> p o j")
            if PW_ENG == "g":
                nc.gpsimd.tensor_scalar(out=w_grp[:, s], in0=src, scalar1=1.0, scalar2=0.0, op0=ALU.mult, op1=ALU.add)
                nc.gpsimd.tensor_scalar(
                    out=bias_f[:, s], in0=bias_bf[:, s], scalar1=1.0, scalar2=0.0, op0=ALU.mult, op1=ALU.add
                )
            else:
                nc.vector.tensor_copy(out=w_grp[:, s], in_=src)
                nc.vector.tensor_copy(out=bias_f[:, s], in_=bias_bf[:, s])

        def prep_w(s):
            nc.vector.quantize_mx(
                out=w_codes[:, s].bitcast(FP8X4), scales=w_scales[:, s],
                in_=w_grp[:, s].rearrange("p o j -> p (o j)"),
            )

        def copy_on(eng, out, in_):
            if eng == "v":
                nc.vector.tensor_copy(out=out, in_=in_)
            else:
                nc.scalar.copy(out=out, in_=in_)


        def misc_bank(st, kind, shape, dtype, name):
            if st < 0 or st >= UNITS + 2:
                kind = "s"
            nm = BANKS[kind][0]
            return ps[nm].tile(shape, dtype, name=name, tag=nm)

        xts = {}

        def qk_group(st, kind, x, b, h, a, cs=(0, 1, 2, 3)):
            src = raws[(x, b, h)]
            if (x, b, h) not in xts:
                t = xt.tile([P, 8 * P], F32, name="xt_%s%d" % (x, h))
                xts[(x, b, h)] = t
            dst = xts[(x, b, h)]
            nt = len(cs)
            bank = misc_bank(st, kind, [P, nt, P], F32, "bank_x")
            trs = [
                (lambda n=n, c=c: nc.tensor.transpose(bank[:, n, :], src[:, a, c, :].bitcast(F32), ident_f[:]))
                for n, c in enumerate(cs)
            ]
            out = dst[:, a * 512 + cs[0] * P:a * 512 + (cs[-1] + 1) * P]
            if x == "q":
                return trs, lambda eng: copy_on(eng, out, bank[:].rearrange("p c t -> p (c t)"))
            return trs, lambda eng: copy_on(
                eng, out.rearrange("p (u t e) -> p u t e", u=nt // 2, e=2), bank[:].rearrange("p (u e) t -> p u t e", e=2)
            )

        GROUPS = [("q", 0, 0), ("k", 0, 0), ("k", 0, 1), ("q", 1, 0), ("k", 1, 0), ("k", 1, 1), ("q", 0, 1), ("q", 1, 1)]
        qk_plan = {0: [(0, 4, "qk"), (0, 5, "pv")], 3: [(0, 6, "qk")], 5: [(0, 7, "qk")]}
        for b in range(1, B):
            for n in range(8):
                qk_plan.setdefault(16 * (b - 1) + 2 * n + QK_PAR, []).append((b, n, "qk"))
        for late in (3, 5):
            if len(qk_plan[late]) > 1:
                qk_plan[late][1] = qk_plan[late][1][:2] + (LATE_KIND,)

        def half(view, e):
            return view.bitcast(BF16).rearrange("p (x e) -> p x e", e=2)[:, :, e]

        vcs = {}

        def v_regroup(b, h, g, u):
            v_grp = vg.tile([P, DH // 2, 4], BF16, name="v_grp", align_bytes=64)
            vcs[("g", b, h, g, u)] = v_grp
            nc.gpsimd.tensor_scalar(
                out=v_grp[:].rearrange("p (x e) j -> p x e j", e=2),
                in0=raws[("v", b, h)][:, g].rearrange("p j (x u e) -> p u x e j", u=2, e=2)[:, u],
                scalar1=1.0, scalar2=0.0, op0=ALU.mult, op1=ALU.add,
            )

        def v_quant(b, h, g, u):
            if (g, u) == (0, 0):
                v_codes = vq.tile([P, 2 * DH], U32, name="v_codes%d" % h, align_bytes=64)
                v_scales = vq.tile([P, 2 * DH], U8, name="v_scales%d" % h, align_bytes=64)
                vcs[("c", b, h)] = (v_codes, v_scales)
            v_codes, v_scales = vcs[("c", b, h)]
            cols = slice((2 * g + u) * P, (2 * g + u + 1) * P)
            nc.vector.quantize_mx(
                out=v_codes[:, cols].bitcast(FP8X4), scales=v_scales[:, cols],
                in_=vcs[("g", b, h, g, u)][:].rearrange("p d j -> p (d j)"),
            )

        V_PLAN = {}
        for n in range(8):
            c = (n // 4, n // 2 % 2, n % 2)
            V_PLAN.setdefault(VQ0 + n // 2, []).append((0,) + c)
            for b in range(1, B):
                V_PLAN.setdefault(16 * (b - 1) + VQB + VQS * n, []).append((b,) + c)
        V_SEQ = [c for st in sorted(V_PLAN) for c in V_PLAN[st]]
        v_next = {V_SEQ[n]: V_SEQ[n + VG_BUFS] for n in range(len(V_SEQ) - VG_BUFS)}

        live = {}

        def unit(i):
            if SWAP and i in (1, 2):
                i = 3 - i
            b, r = divmod(i, 16)
            return b, r // 2, r % 2

        def pair_of(i):
            b, t, h = unit(i)
            return 8 * b + t, h

        def stage_a(i):
            b, t, h = unit(i)
            qt = xts[("q", b, h)]
            kt = xts[("k", b, h)]
            banks = []
            mms = []
            for g in range(2):
                s_ps = ps["s"].tile([P, 512], F32, name="s_ps", tag="s")
                banks.append(s_ps)
                for e in range(2):
                    mms.append(
                        lambda s_ps=s_ps, g=g, e=e: nc.tensor.matmul(
                            out=s_ps[:],
                            lhsT=half(qt[:, t * P:(t + 1) * P], e),
                            rhs=half(kt[:, g * 512:(g + 1) * 512], e),
                            start=(e == 0), stop=(e == 1),
                        )
                    )
            live[("s", i)] = banks
            return mms

        def stage_b(i):
            banks = live[("s", i)]
            m2 = st4.tile([P, 2], F32, name="m2")
            for g in range(2):
                nc.vector.reduce_max(out=m2[:, g:g + 1], in_=banks[g][:], axis=AX.X)
            live[("m2", i)] = m2

        def stage_b2(i):
            m2 = live[("m2", i)]
            negmax = st4.tile([P, 1], F32, name="negmax")
            (nc.vector if NEG_ENG == "v" else nc.gpsimd).tensor_scalar(
                out=negmax[:], in0=m2[:, 0:1], scalar1=m2[:, 1:2], scalar2=-SCALE, op0=ALU.max, op1=ALU.mult
            )
            live[("negmax", i)] = negmax

        def stage_c(i):
            banks = live[("s", i)]
            negmax = live[("negmax", i)]
            u, h = pair_of(i)
            if SUM2:
                if ("rs", u // 2) not in live:
                    rs = st4.tile([P, 8], F32, name="rs")
                    live[("rs", u // 2)] = rs
                rs = live[("rs", u // 2)]
            else:
                if h == 0:
                    rs = st4.tile([P, 4], F32, name="rs")
                    live[("rs", u)] = rs
                rs = live[("rs", u)]
            e_sb = ep.tile([P, 2, 512], BF16, name="e_sb")
            for g in range(2):
                col = h * 2 + g + (4 * (u % 2) if SUM2 else 0)
                nc.scalar.activation(
                    out=e_sb[:, g, :], in_=banks[g][:], func=ACT.Exp,
                    bias=negmax[:, 0:1], scale=SCALE, accum_out=rs[:, col:col + 1],
                )
            live[("e", i)] = e_sb

        def stage_d(i):
            words = live[("e", i)][:].rearrange("p g m -> p (g m)").bitcast(F32)
            et_ps = misc_bank(0, "et", [P, 4, P], F32, "et_ps")
            live[("et", i)] = et_ps
            return [
                (lambda x=x: nc.tensor.transpose(et_ps[:, x, :], words[:, x * P:(x + 1) * P], ident_f[:])) for x in range(4)
            ]

        def stage_e(i, eng):
            et_ps = live[("et", i)]
            eg = gp.tile([P, 2, P, 2], F32, name="eg%d" % pair_of(i)[1], align_bytes=64)
            copy_on(eng, eg[:], et_ps[:].rearrange("p (g u) q -> p g q u", u=2))
            live[("eg",) + pair_of(i)] = eg

        def stage_sum(u):
            if SUM2:
                if u % 2 == 0:
                    return
                rs = live[("rs", u // 2)]
                rsum = st4.tile([P, 4], F32, name="rsum")
                live[("rsum", u // 2)] = rsum
                nc.vector.tensor_reduce(out=rsum[:], in_=rs[:].rearrange("p (h g) -> p h g", g=2), axis=AX.X, op=ALU.add)
                return
            rs = live[("rs", u)]
            rsum = st4.tile([P, 2], F32, name="rsum")
            live[("rsum", u)] = rsum
            if SUM_ENG == "v":
                nc.vector.tensor_reduce(out=rsum[:], in_=rs[:].rearrange("p (h g) -> p h g", g=2), axis=AX.X, op=ALU.add)
            else:
                two = rs[:].rearrange("p (h g) -> p h g", g=2)
                nc.gpsimd.tensor_tensor(out=rsum[:], in0=two[:, :, 0], in1=two[:, :, 1], op=ALU.add)

        def stage_recip(u):
            if SUM2:
                if u % 2 == 0:
                    return
                rinv = st4.tile([P, 4], F32, name="rinv")
                live[("rinv", u - 1)] = rinv[:, 0:2]
                live[("rinv", u)] = rinv[:, 2:4]
                nc.vector.reciprocal(out=rinv[:], in_=live[("rsum", u // 2)][:])
                return
            rinv = st4.tile([P, 2], F32, name="rinv")
            live[("rinv", u)] = rinv
            nc.vector.reciprocal(out=rinv[:], in_=live[("rsum", u)][:])

        def stage_g(u):
            e_codes = gp.tile([P, 4 * P], U32, name="e_codes", align_bytes=64)
            e_scales = gp.tile([P, 4 * P], U8, name="e_scales", align_bytes=64)
            live[("ec", u)] = (e_codes, e_scales)
            return lambda h: nc.vector.quantize_mx(
                out=e_codes[:, h * 256:(h + 1) * 256].bitcast(FP8X4), scales=e_scales[:, h * 256:(h + 1) * 256],
                in_=live[("eg", u, h)][:].rearrange("p g q u -> p (g q u)").bitcast(BF16),
            )

        def stage_h(st, u):
            b = u // 8
            e_codes, e_scales = live[("ec", u)]
            pv = misc_bank(st, "pv", [P, 2, DH], F32, "pv")
            live[("pv", u)] = pv
            mx = []
            for h in range(H):
                v_codes, v_scales = vcs[("c", b, h)]
                for g in range(2):
                    c0 = (h * 2 + g) * P
                    mx.append(
                        lambda h=h, g=g, c0=c0, v_codes=v_codes, v_scales=v_scales: nc.tensor.matmul_mx(
                            out=pv[:, h, :],
                            lhsT=e_codes[:, c0:c0 + P].bitcast(FP8X4), lhsT_scale=e_scales[:, c0:c0 + P],
                            rhs=v_codes[:, g * DH:(g + 1) * DH].bitcast(FP8X4),
                            rhs_scale=v_scales[:, g * DH:(g + 1) * DH],
                            start=(g == 0), stop=(g == 1),
                        )
                    )
            return mx

        def stage_i(u):
            pv = live[("pv", u)]
            attn = ap3.tile([P, H * DH], BF16, name="attn")
            live[("attn", u)] = attn
            dst = attn[:].rearrange("p (u h x) -> p u h x", u=2, h=H)
            def go(h, eng):
                rinv = live[("rinv", u)]
                if eng == "s":
                    nc.scalar.activation(
                        out=dst[:, :, h, :], in_=pv[:, h, :].rearrange("p (u x) -> p u x", u=2), func=ACT.Copy,
                        scale=rinv[:, h:h + 1],
                    )
                else:
                    nc.vector.tensor_scalar(
                        out=dst[:, :, h, :], in0=pv[:, h, :].rearrange("p (u x) -> p u x", u=2),
                        scalar1=rinv[:, h:h + 1], scalar2=None, op0=ALU.mult,
                    )
            return go

        def stage_j(st, u):
            words = live[("attn", u)][:].bitcast(F32)
            at_ps = misc_bank(st, "at", [P, 2, P], F32, "at_ps")
            live[("at", u)] = at_ps
            return [
                (lambda x=x: nc.tensor.transpose(at_ps[:, x, :], words[:, x * P:(x + 1) * P], ident_f[:]))
                for x in range(2)
            ]

        def stage_k(u):
            eng = "v" if K_ENG == "v" or u % K_V == K_V - 1 else "s"
            at_ps = live[("at", u)]
            ag = ap3.tile([P, P, 2], F32, name="ag", align_bytes=64)
            copy_on(eng, ag[:], at_ps[:].rearrange("p u q -> p q u"))
            live[("ag", u)] = ag

        def stage_l(u):
            ag = live[("ag", u)]
            a_codes = ap3.tile([P, P], U32, name="a_codes", align_bytes=64)
            a_scales = ap3.tile([P, P], U8, name="a_scales", align_bytes=64)
            nc.vector.quantize_mx(
                out=a_codes[:].bitcast(FP8X4), scales=a_scales[:],
                in_=ag[:].rearrange("p q u -> p (q u)").bitcast(BF16),
            )
            live[("ac", u)] = (a_codes, a_scales)

        def stage_m(st, u):
            s = (u % 8) // 4
            a_codes, a_scales = live[("ac", u)]
            o_ps = misc_bank(st, "o", [P, D], F32, "o_ps")
            live[("o", u)] = o_ps
            return [
                lambda: nc.tensor.matmul_mx(
                    out=o_ps[:],
                    lhsT=a_codes[:].bitcast(FP8X4), lhsT_scale=a_scales[:],
                    rhs=w_codes[:, s, :].bitcast(FP8X4), rhs_scale=w_scales[:, s, :],
                    start=True, stop=True,
                )
            ]

        def stage_n(u):
            b = u // 8
            s = (u % 8) // 4
            o_ps = live[("o", u)]
            o_sb = ap3.tile([P, D], F32, name="o_sb", bufs=8)
            nc.vector.tensor_tensor(out=o_sb[:], in0=o_ps[:], in1=bias_f[:, s, :], op=ALU.add)
            nc.sync.dma_start(out=outs[s][b, (u % 4) * P:(u % 4 + 1) * P, :], in_=o_sb[:])

        def due(st, off):
            if st >= off and (st - off) % 2 == 0 and (st - off) // 2 < PAIRS:
                return (st - off) // 2
            return None

        if LOADS == 0:
            for n in range(4):
                x, h, a = GROUPS[n]
                trs, evac = qk_group(-1, "qk", x, 0, h, a)
                for f in trs:
                    f()
                evac("v" if n % 2 == 0 else "s")
        else:
            if WARM[0]:
                zeros = consts.tile([P, 512], BF16)
                nc.vector.memset(zeros[:], 0.0)

            def warm(n):
                for k in range(n):
                    scratch = ps["et"].tile([P, 512], F32, name="scratch", tag="et")
                    nc.tensor.matmul(out=scratch[:], lhsT=zeros[:, 0:P], rhs=zeros[:], start=True, stop=True)

            warm(WARM[0])
            for k, (x, a, cs, eng) in enumerate((("q", 0, (0,), "v"), ("k", 0, (0, 1), "v"), ("k", 0, (2, 3), "s"), ("k", 1, (0, 1), "v"), ("k", 1, (2, 3), "s"))):
                if k == 3:
                    warm(WARM[1])
                trs, evac = qk_group(-1, "qk", x, 0, 0, a, cs)
                for f in trs:
                    f()
                evac(eng)

        for n in range(VG_BUFS):
            v_regroup(*V_SEQ[n])

        for st in range(UNITS + max(OFF_M, OFF_N) + 1):
            b16, r16 = divmod(st, 16)
            ug, ur, uh, ui = due(st, OFF_G), due(st, OFF_R), due(st, OFF_H), due(st, OFF_I)
            usum = due(st, OFF_SUM)
            uj, uk, ul, um, un = due(st, OFF_J), due(st, OFF_K), due(st, OFF_L), due(st, OFF_M), due(st, OFF_N)
            pe = {"a0": [], "D": [], "Q": [], "J": [], "H": [], "M": []}
            mms = stage_a(st) if st < UNITS else [None] * 4
            for n in range(4):
                pe["a%d" % n] = [mms[n]] if mms[n] else []
            evacs = []
            if 0 <= st - OFF_D < UNITS:
                pe["D"] = stage_d(st - OFF_D)
            for n in range(4):
                pe["D%d" % n] = pe["D"][n:n + 1]
            todo = [(b, kind) + GROUPS[gi] for b, gi, kind in qk_plan.get(st, [])]
            if st == 0 and LOADS == 2:
                todo = [(0, "qk", "q", 0, 0, (1, 2, 3)), (0, "pv", "k", 1, 0), (0, "et", "k", 1, 1), (0, "et", "q", 1, 0)]
            elif st == 0 and LOADS:
                todo = [(0, "qk", "k", 1, 0), (0, "pv", "k", 1, 1), (0, "et", "q", 1, 0), (0, "et", "q", 0, 0, (1, 2, 3))]
            for b, kind, x, h, a, *cs in todo:
                trs, evac = qk_group(st, kind, x, b, h, a, *cs)
                pe["Q"] += trs
                evacs.append(evac)
            if uj is not None:
                pe["J"] = stage_j(st, uj)
            if uh is not None:
                pe["H"] = stage_h(st, uh)
            if um is not None:
                pe["M"] = stage_m(st, um)
            for nm in ("Q", "J", "H"):
                for n in range(4):
                    pe["%s%d" % (nm, n)] = pe[nm][n:n + 1]
            pe["Q4"] = pe["Q"][4:]
            for key in PE_ORDER:
                for f in pe[key]:
                    f()
            if st < UNITS and r16 == 7 and b16 + 2 < B:
                load_batch(b16 + 2)
            if st < UNITS:
                stage_b(st)
            go = stage_i(ui) if ui is not None else None
            i_eng = TAIL_I if st >= UNITS else ("s", "v") if ui is not None and ui % I_V == I_V - 1 else I_ENG
            gq = stage_g(ug) if ug is not None else None

            def vec(key):
                if key == "sum" and usum is not None:
                    stage_sum(usum)
                if key == "recip" and ur is not None:
                    stage_recip(ur)
                if key == "K" and uk is not None and (K_ENG == "v" or uk % K_V == K_V - 1):
                    stage_k(uk)
                if key == "L" and ul is not None:
                    stage_l(ul)
                if key == "N" and un is not None:
                    stage_n(un)
                if key in ("G0", "G1") and gq:
                    gq(int(key[1]))
                if key == "I":
                    for h in range(2):
                        if go and i_eng[h] == "v":
                            go(h, "v")
                if key == "Q" and Q_ENG == "v":
                    for evac in evacs:
                        evac("s" if st == 0 and EARLY_Q == 0 else "v")

            for key in FILL:
                if not (st == 0 and LOADS):
                    vec(key)
            if st < UNITS:
                stage_b2(st)
            for key in S_ORDER:
                if key == "E" and 0 <= st - OFF_E < UNITS:
                    stage_e(st - OFF_E, "v" if st == UNITS + 1 else E_ENG[st % 2])
                if key == "I" and go:
                    for h in range(2):
                        if i_eng[h] == "s":
                            go(h, "s")
                if key == "K" and uk is not None and K_ENG == "s" and uk % K_V != K_V - 1:
                    stage_k(uk)
                if key == "C" and st < UNITS:
                    if st == 0 and LOADS == 2:
                        pass
                    elif st == 0 and LOADS:
                        evacs[0]("s")
                        evacs[1]("s")
                    elif st == 0 and EARLY_Q == 1:
                        evacs[0]("s")
                        evacs = evacs[1:]
                    stage_c(st)
                if key == "Q" and Q_ENG == "s":
                    for evac in evacs:
                        evac("s")
            if st == 0 and LOADS == 2:
                evacs[0]("v")
                evacs[1]("s")
                evacs[2]("s")
                late_q = evacs[3]
            elif st == 1 and LOADS == 2:
                late_q("v")
            elif st == 0 and LOADS:
                evacs[2]("v")
                evacs[3]("v")
            for key in V_ORDER:
                if not (st == 0 and LOADS):
                    vec(key)
            for c in V_PLAN.get(st, []):
                v_quant(*c)
                if c in v_next:
                    v_regroup(*v_next[c])
            for s in range(2):
                if st == PW[s]:
                    prep_w0(s)
                if st == PW[s] + 3:
                    prep_w(s)
